import numpy as np
import ml_dtypes


def mxq(x, axis, fmt="e4m3"):
    dtype, down = {"e4m3": (ml_dtypes.float8_e4m3fn, 7), "e5m2": (ml_dtypes.float8_e5m2, 14)}[fmt]
    v = np.moveaxis(np.asarray(x, np.float32).astype(ml_dtypes.bfloat16).astype(np.float64), axis, -1)
    blocks = v.reshape(v.shape[:-1] + (-1, 32))
    amax = np.abs(blocks).max(-1, keepdims=True)
    byte = np.maximum(np.where(amax > 0, np.frexp(amax)[1] - 1 + 127, 0) - down, 1)
    scale = np.exp2(byte - 127.0)
    codes = (blocks / scale).astype(np.float32).astype(dtype).astype(np.float64)
    return np.moveaxis((codes * scale).reshape(v.shape), -1, axis)


WIDE = False


def mx_kscale(k):
    if not WIDE:
        return np.ones(k)
    levels = np.array([10, -10, 5, -5, 0])
    a = np.random.permutation(np.resize(levels, k // 512 * 4)).reshape(k // 512, 4)
    idx = np.arange(k)
    return np.exp2(a[idx // 512, idx % 128 // 32])


BF16 = ml_dtypes.bfloat16


def bf(x):
    return np.asarray(x, np.float32).astype(BF16)


def f64(x):
    return np.asarray(x).astype(np.float64)


E2M1 = np.array([0.0, 0.5, 1.0, 1.5, 2.0, 3.0, 4.0, 6.0, -0.0, -0.5, -1.0, -1.5, -2.0, -3.0, -4.0, -6.0])


def pack_weight(w, fmt):
    k, n = w.shape
    w = f64(bf(w)).reshape(k // 32, 32, n)
    amax = np.abs(w).max(1)
    if fmt == "e4m3":
        byte = np.frexp(amax)[1] - 1 + 127 - 7
    else:
        mant, ex = np.frexp(amax / 6.0)
        byte = np.where(mant > 0.5, ex, ex - 1) + 127
    byte = np.clip(np.where(amax > 0, byte, 1), 1, 254)
    scaled = (w * np.exp2(127.0 - byte)[:, None, :]).reshape(k, n).astype(np.float32)
    by_word = np.ascontiguousarray(scaled.reshape(k // 512, 128, 4, n).transpose(0, 1, 3, 2))
    if fmt == "e4m3":
        words = by_word.astype(ml_dtypes.float8_e4m3fn).view(np.uint8)
    else:
        c = by_word.astype(ml_dtypes.float4_e2m1fn).view(np.uint8) & 0xF
        words = c[..., 0::2] | (c[..., 1::2] << 4)
    return np.ascontiguousarray(words), np.ascontiguousarray(byte.astype(np.uint8).reshape(k // 512, 16, n))


def unpack_weight(words, scales, fmt):
    g, p, n, _ = words.shape
    if fmt == "e4m3":
        vals = np.ascontiguousarray(words).view(ml_dtypes.float8_e4m3fn).astype(np.float64)
    else:
        nib = np.empty((g, p, n, 4), np.uint8)
        nib[..., 0::2] = words & 0xF
        nib[..., 1::2] = words >> 4
        vals = E2M1[nib]
    vals = vals * np.repeat(np.exp2(scales.astype(np.float64) - 127.0), 8, axis=1)[..., None]
    return vals.transpose(0, 1, 3, 2).reshape(g * 512, n)


B, L, D, F = 2, 128, 512, 16384
FMT = "e4m3"


def silu(z):
    return z / (1.0 + np.exp(-z))


def sigmoid(z):
    return 1.0 / (1.0 + np.exp(-z))


def setup_inputs():
    s = mx_kscale(D)
    x = bf(np.random.standard_normal((B, L, D)) * s)
    W1_words, W1_scales = pack_weight(np.random.standard_normal((D, F)) / np.sqrt(D) / s[:, None], FMT)
    b1 = bf(np.random.standard_normal(F) * 0.3)
    W2g_words, W2g_scales = pack_weight(np.random.standard_normal((F, D)) * 2.4 / np.sqrt(F), FMT)
    b2g = bf(np.random.standard_normal(D) * 0.3)
    Wv_words, Wv_scales = pack_weight(np.random.standard_normal((D, D)) * 1.8 / np.sqrt(D) / s[:, None], FMT)
    bv = bf(np.random.standard_normal(D) * 0.3)
    return {
        "x": x,
        "W1_words": W1_words,
        "W1_scales": W1_scales,
        "b1": b1,
        "W2g_words": W2g_words,
        "W2g_scales": W2g_scales,
        "b2g": b2g,
        "Wv_words": Wv_words,
        "Wv_scales": Wv_scales,
        "bv": bv,
    }


def reference(x, W1_words, W1_scales, b1, W2g_words, W2g_scales, b2g, Wv_words, Wv_scales, bv):
    xq = mxq(f64(x), 2, "e4m3")
    h = silu((xq @ unpack_weight(W1_words, W1_scales, FMT)) + f64(b1))
    g = (mxq(h, 2, "e4m3") @ unpack_weight(W2g_words, W2g_scales, FMT)) + f64(b2g)
    return ((xq @ unpack_weight(Wv_words, Wv_scales, FMT)) + f64(bv)) * sigmoid(g)

@@ -1,0 +1,248 @@
+from contextlib import ExitStack
+
+import concourse.mybir as mybir
+from concourse.masks import make_identity
+
+F32 = mybir.dt.float32
+BF16 = mybir.dt.bfloat16
+I32 = mybir.dt.int32
+U32 = mybir.dt.uint32
+U8 = mybir.dt.uint8
+FP8X4 = mybir.dt.float8_e4m3fn_x4
+ACT = mybir.ActivationFunctionType
+ADD = mybir.AluOpType.add
+MULT = mybir.AluOpType.mult
+
+P = 128
+TOKENS = 256
+TOKEN_TILES = TOKENS // P
+D = 512
+F = 16384
+GROUPS = F // D
+ROUND = 2
+ROUNDS = GROUPS // ROUND
+WEIGHT_BUFS = 8
+QUARTER = F // 4
+
+FLOPS = 2 * TOKENS * (D * F + F * D + D * D)
+
+
+def tile_selectivemixing_pa_k_kernel(
+    tc, x, W1_words, W1_scales, b1, W2g_words, W2g_scales, b2g, Wv_words, Wv_scales, bv, out
+):
+    nc = tc.nc
+    x_rows = x.flatten_outer_dims()
+    out_rows = out.flatten_outer_dims()
+    w1_dram = W1_words[0].rearrange("p n t -> p (n t)").bitcast(I32)
+
+    with ExitStack() as stack:
+        consts = stack.enter_context(tc.tile_pool(name="consts", bufs=1))
+        weights = stack.enter_context(tc.tile_pool(name="weights", bufs=WEIGHT_BUFS))
+        work = stack.enter_context(tc.tile_pool(name="work", bufs=4))
+        psum_acc = stack.enter_context(tc.psum_pool(name="psum_acc", bufs=1))
+        psum_z = stack.enter_context(tc.psum_pool(name="psum_z", bufs=2 * ROUND))
+        psum_flip = stack.enter_context(tc.psum_pool(name="psum_flip", bufs=ROUND))
+
+        w1_planes = consts.tile([P, QUARTER], U8, align_bytes=64)
+        bias_rows = consts.tile([P, D], BF16)
+        w2_planes = consts.tile([P, GROUPS, D], U8, align_bytes=64)
+        wv_plane = consts.tile([P, D], U8, align_bytes=64)
+        nc.vector.memset(w1_planes[:].bitcast(I32), 0)
+        nc.vector.memset(bias_rows[:].bitcast(I32), 0)
+        nc.vector.memset(w2_planes[:].bitcast(I32), 0)
+        nc.vector.memset(wv_plane[:].bitcast(I32), 0)
+
+        ident_f32 = consts.tile([P, P], F32)
+        ident_bf16 = consts.tile([P, P], BF16)
+        make_identity(nc, ident_bf16[:])
+        make_identity(nc, ident_f32[:])
+
+        nc.scalar.dma_start(out=bias_rows[0:GROUPS, :], in_=b1.rearrange("(g n) -> g n", n=D))
+        nc.scalar.dma_start(out=bias_rows[GROUPS : GROUPS + 1, :], in_=b2g.rearrange("(o n) -> o n", o=1))
+        nc.scalar.dma_start(out=bias_rows[GROUPS + 1 : GROUPS + 2, :], in_=bv.rearrange("(o n) -> o n", o=1))
+        x_sb = consts.tile([P, TOKEN_TILES, D], BF16)
+        nc.sync.dma_start(out=x_sb[:], in_=x_rows.rearrange("(t p) d -> p t d", p=P))
+        w1_scale_quarters = W1_scales[0].bitcast(I32).rearrange("q (k n) -> k q n", k=4)
+        for quadrant in range(4):
+            nc.sync.dma_start(
+                out=w1_planes[32 * quadrant : 32 * quadrant + 16, :].bitcast(I32),
+                in_=w1_scale_quarters[:, 4 * quadrant : 4 * quadrant + 4, :],
+            )
+
+        w1_tiles = {}
+        w2_tiles = {}
+
+        def load_w1(r):
+            w1 = weights.tile([P, ROUND * D], U32, align_bytes=64)
+            nc.sync.dma_start(out=w1[:].bitcast(I32), in_=w1_dram[:, ROUND * D * r : ROUND * D * (r + 1)])
+            w1_tiles[r] = w1
+
+        def load_w2(r):
+            w2 = weights.tile([P, ROUND, D], U32, align_bytes=64)
+            nc.sync.dma_start(
+                out=w2[:].bitcast(I32),
+                in_=W2g_words[ROUND * r : ROUND * (r + 1)].rearrange("g p n t -> p g (n t)").bitcast(I32),
+            )
+            w2_tiles[r] = w2
+
+        LAG = 3
+        for r in range(LAG):
+            load_w1(r)
+        for quadrant in range(4):
+            nc.sync.dma_start(
+                out=w2_planes[32 * quadrant : 32 * quadrant + 4, :, :].bitcast(I32),
+                in_=W2g_scales[:, 4 * quadrant : 4 * quadrant + 4, :].bitcast(I32).rearrange("g r n -> r g n"),
+            )
+        for r in range(ROUNDS):
+            load_w2(r)
+            if r + LAG < ROUNDS:
+                load_w1(r + LAG)
+        wv_words = consts.tile([P, D], U32, align_bytes=64)
+        nc.sync.dma_start(out=wv_words[:].bitcast(I32), in_=Wv_words[0].rearrange("p n t -> p (n t)").bitcast(I32))
+        for quadrant in range(4):
+            nc.sync.dma_start(
+                out=wv_plane[32 * quadrant : 32 * quadrant + 4, :].bitcast(I32),
+                in_=Wv_scales[0][4 * quadrant : 4 * quadrant + 4, :].bitcast(I32),
+            )
+
+        def flip(words):
+            flipped = psum_flip.tile([P, TOKEN_TILES, 2, P], F32, tag="flip")
+            for t in range(TOKEN_TILES):
+                for u in range(2):
+                    nc.tensor.transpose(flipped[:, t, u, :], words[:, t, u, :], ident_f32[:])
+            return flipped
+
+        def regroup(flipped):
+            grouped = work.tile([P, TOKENS * 4], BF16, align_bytes=64)
+            nc.scalar.copy(
+                out=grouped[:].bitcast(F32).rearrange("p (t k u) -> p t k u", t=TOKEN_TILES, u=2),
+                in_=flipped[:].rearrange("p t u k -> p t k u"),
+            )
+            return grouped
+
+        def quantise(grouped, codes, plane):
+            nc.vector.quantize_mx(out=codes[:].bitcast(FP8X4), scales=plane[:], in_=grouped[:])
+
+        x_codes = consts.tile([P, TOKENS], U32, align_bytes=64)
+        x_plane = consts.tile([P, TOKENS], U8, align_bytes=64)
+        quantise(regroup(flip(x_sb[:].bitcast(F32).rearrange("p t (q u) -> p t u q", u=2))), x_codes, x_plane)
+
+        b1_all = consts.tile([P, GROUPS, D], BF16)
+        tail_bias = consts.tile([P, 2, D], BF16)
+        for c in range(0, GROUPS + 2, 2):
+            spread = psum_flip.tile([P, 2, D], BF16, tag="flip")
+            for i in range(2):
+                nc.tensor.matmul(
+                    out=spread[:, i, :],
+                    lhsT=ident_bf16[:, c + i : c + i + 1].to_broadcast([P, P]),
+                    rhs=bias_rows[:],
+                    start=True,
+                    stop=True,
+                )
+            if c < GROUPS:
+                dst = b1_all[:, c : c + 2, :].bitcast(F32).rearrange("p i (u q) -> p i u q", u=2)
+                src = spread[:].bitcast(F32).rearrange("p i (q u) -> p i u q", u=2)
+            else:
+                dst = tail_bias[:]
+                src = spread[:]
+            if c % 4 == 0:
+                nc.vector.tensor_copy(out=dst, in_=src)
+            else:
+                nc.scalar.copy(out=dst, in_=src)
+
+        h_tiles = {}
+        flipped_tiles = {}
+        grouped_tiles = {}
+        h_codes = {}
+        h_planes = {}
+        acc = [psum_acc.tile([P, D], F32, name="acc%d" % t) for t in range(TOKEN_TILES)]
+
+        def first_layer(r):
+            for g in range(ROUND * r, ROUND * (r + 1)):
+                offset = 4 * (g * D // QUARTER)
+                cols = g * D % QUARTER
+                zb = work.tile([P, TOKEN_TILES, D], F32)
+                for t in range(TOKEN_TILES):
+                    z = psum_z.tile([P, D], F32, tag="z")
+                    nc.tensor.matmul_mx(
+                        out=z[:],
+                        lhsT=x_codes[:, P * t : P * (t + 1)].bitcast(FP8X4),
+                        lhsT_scale=x_plane[:, P * t : P * (t + 1)],
+                        rhs=w1_tiles[r][:, D * (g % ROUND) : D * (g % ROUND + 1)].bitcast(FP8X4),
+                        rhs_scale=w1_planes[offset:P, cols : cols + D],
+                        start=True,
+                        stop=True,
+                    )
+                    nc.vector.tensor_tensor(
+                        out=zb[:, t, :].rearrange("p (u q e) -> p u q e", u=2, e=2),
+                        in0=z[:].rearrange("p (q u e) -> p u q e", u=2, e=2),
+                        in1=b1_all[:, g, :].rearrange("p (u q e) -> p u q e", u=2, e=2),
+                        op=ADD,
+                    )
+                h = work.tile([P, TOKEN_TILES, D], BF16, bufs=6)
+                nc.scalar.activation(out=h[:], in_=zb[:], func=ACT.Silu)
+                h_tiles[g] = h
+
+        def flip_round(r):
+            for g in range(ROUND * r, ROUND * (r + 1)):
+                flipped_tiles[g] = flip(h_tiles[g][:].bitcast(F32).rearrange("p t (u q) -> p t u q", u=2))
+            for g in range(ROUND * r, ROUND * (r + 1)):
+                grouped_tiles[g] = regroup(flipped_tiles[g])
+
+        def quantise_round(r):
+            for g in range(ROUND * r, ROUND * (r + 1)):
+                codes = work.tile([P, TOKENS], U32, align_bytes=64, bufs=6)
+                plane = work.tile([P, TOKENS], U8, align_bytes=64, bufs=6)
+                quantise(grouped_tiles[g], codes, plane)
+                h_codes[g] = codes
+                h_planes[g] = plane
+
+        def second_layer(r):
+            for g in range(ROUND * r, ROUND * (r + 1)):
+                for t in range(TOKEN_TILES):
+                    nc.tensor.matmul_mx(
+                        out=acc[t][:],
+                        lhsT=h_codes[g][:, P * t : P * (t + 1)].bitcast(FP8X4),
+                        lhsT_scale=h_planes[g][:, P * t : P * (t + 1)],
+                        rhs=w2_tiles[r][:, g % ROUND, :].bitcast(FP8X4),
+                        rhs_scale=w2_planes[:, g, :],
+                        start=(g == 0),
+                        stop=(g == GROUPS - 1),
+                    )
+
+        values = consts.tile([P, TOKEN_TILES, D], F32)
+
+        def value_path():
+            for t in range(TOKEN_TILES):
+                v = psum_z.tile([P, D], F32, tag="z")
+                nc.tensor.matmul_mx(
+                    out=v[:],
+                    lhsT=x_codes[:, P * t : P * (t + 1)].bitcast(FP8X4),
+                    lhsT_scale=x_plane[:, P * t : P * (t + 1)],
+                    rhs=wv_words[:].bitcast(FP8X4),
+                    rhs_scale=wv_plane[:],
+                    start=True,
+                    stop=True,
+                )
+                nc.vector.tensor_tensor(out=values[:, t, :], in0=v[:], in1=tail_bias[:, 1, :], op=ADD)
+
+        for r in range(ROUNDS + LAG):
+            if r < ROUNDS:
+                first_layer(r)
+            if r == ROUNDS:
+                value_path()
+            if r >= LAG:
+                second_layer(r - LAG)
+            if 1 <= r <= ROUNDS:
+                flip_round(r - 1)
+            if 2 <= r <= ROUNDS + 1:
+                quantise_round(r - 2)
+
+        for t in range(TOKEN_TILES):
+            gate = work.tile([P, D], F32, bufs=2)
+            nc.vector.tensor_tensor(out=gate[:], in0=acc[t][:], in1=tail_bias[:, 0, :], op=ADD)
+            opened = work.tile([P, D], F32, bufs=2)
+            nc.scalar.activation(out=opened[:], in_=gate[:], func=ACT.Sigmoid)
+            result = work.tile([P, D], F32, bufs=2)
+            nc.vector.tensor_tensor(out=result[:], in0=values[:, t, :], in1=opened[:], op=MULT)
+            nc.sync.dma_start(out=out_rows[P * t : P * (t + 1), :], in_=result[:])

@@ -21,8 +21,10 @@ F = 16384
 GROUPS = F // D
 ROUND = 2
 ROUNDS = GROUPS // ROUND
+LAG = 3
 WEIGHT_BUFS = 8
 QUARTER = F // 4
+BIAS_ROWS = GROUPS + 2
 
 FLOPS = 2 * TOKENS * (D * F + F * D + D * D)
 
@@ -42,24 +44,27 @@ def tile_selectivemixing_pa_k_kernel(
         psum_acc = stack.enter_context(tc.psum_pool(name="psum_acc", bufs=1))
         psum_z = stack.enter_context(tc.psum_pool(name="psum_z", bufs=2 * ROUND))
         psum_flip = stack.enter_context(tc.psum_pool(name="psum_flip", bufs=ROUND))
+        stack.enter_context(tc.manual_schedule())
 
         w1_planes = consts.tile([P, QUARTER], U8, align_bytes=64)
         bias_rows = consts.tile([P, D], BF16)
         w2_planes = consts.tile([P, GROUPS, D], U8, align_bytes=64)
         wv_plane = consts.tile([P, D], U8, align_bytes=64)
+        zero = consts.tile([P, 1], F32)
+        warm = consts.tile([P, 1], F32)
+        nc.vector.memset(zero[:], 0.0)
         nc.vector.memset(w1_planes[:].bitcast(I32), 0)
         nc.vector.memset(bias_rows[:].bitcast(I32), 0)
         nc.vector.memset(w2_planes[:].bitcast(I32), 0)
         nc.vector.memset(wv_plane[:].bitcast(I32), 0)
 
         ident_f32 = consts.tile([P, P], F32)
-        ident_bf16 = consts.tile([P, P], BF16)
-        make_identity(nc, ident_bf16[:])
         make_identity(nc, ident_f32[:])
 
         nc.scalar.dma_start(out=bias_rows[0:GROUPS, :], in_=b1.rearrange("(g n) -> g n", n=D))
         nc.scalar.dma_start(out=bias_rows[GROUPS : GROUPS + 1, :], in_=b2g.rearrange("(o n) -> o n", o=1))
         nc.scalar.dma_start(out=bias_rows[GROUPS + 1 : GROUPS + 2, :], in_=bv.rearrange("(o n) -> o n", o=1))
+        nc.scalar.activation(out=warm[:], in_=zero[:], func=ACT.Silu)
         x_sb = consts.tile([P, TOKEN_TILES, D], BF16)
         nc.sync.dma_start(out=x_sb[:], in_=x_rows.rearrange("(t p) d -> p t d", p=P))
         w1_scale_quarters = W1_scales[0].bitcast(I32).rearrange("q (k n) -> k q n", k=4)
@@ -85,7 +90,6 @@ def tile_selectivemixing_pa_k_kernel(
             )
             w2_tiles[r] = w2
 
-        LAG = 3
         for r in range(LAG):
             load_w1(r)
         for quadrant in range(4):
@@ -112,9 +116,9 @@ def tile_selectivemixing_pa_k_kernel(
                     nc.tensor.transpose(flipped[:, t, u, :], words[:, t, u, :], ident_f32[:])
             return flipped
 
-        def regroup(flipped):
+        def regroup(flipped, copy):
             grouped = work.tile([P, TOKENS * 4], BF16, align_bytes=64)
-            nc.scalar.copy(
+            copy(
                 out=grouped[:].bitcast(F32).rearrange("p (t k u) -> p t k u", t=TOKEN_TILES, u=2),
                 in_=flipped[:].rearrange("p t u k -> p t k u"),
             )
@@ -123,35 +127,42 @@ def tile_selectivemixing_pa_k_kernel(
         def quantise(grouped, codes, plane):
             nc.vector.quantize_mx(out=codes[:].bitcast(FP8X4), scales=plane[:], in_=grouped[:])
 
+        bias_words = bias_rows[:].bitcast(F32).rearrange("c (q u) -> c u q", u=2)
+        bias_flipped = psum_flip.tile([P, 2, P], F32, tag="flip")
+        for u in range(2):
+            nc.tensor.transpose(bias_flipped[:, u, :], bias_words[:, u, :], ident_f32[:])
+        bias_cols = consts.tile([P, 2, P], F32)
+        nc.scalar.copy(out=bias_cols[:], in_=bias_flipped[:])
+
         x_codes = consts.tile([P, TOKENS], U32, align_bytes=64)
         x_plane = consts.tile([P, TOKENS], U8, align_bytes=64)
-        quantise(regroup(flip(x_sb[:].bitcast(F32).rearrange("p t (q u) -> p t u q", u=2))), x_codes, x_plane)
+        x_flipped = flip(x_sb[:].bitcast(F32).rearrange("p t (q u) -> p t u q", u=2))
+        x_grouped = regroup(x_flipped, nc.vector.tensor_copy)
+        quantise(x_grouped, x_codes, x_plane)
 
         b1_all = consts.tile([P, GROUPS, D], BF16)
         tail_bias = consts.tile([P, 2, D], BF16)
-        for c in range(0, GROUPS + 2, 2):
-            spread = psum_flip.tile([P, 2, D], BF16, tag="flip")
+        for c in range(0, BIAS_ROWS, 2):
+            spread = psum_z.tile([P, 2, 2, P], F32, tag="z")
             for i in range(2):
-                nc.tensor.matmul(
-                    out=spread[:, i, :],
-                    lhsT=ident_bf16[:, c + i : c + i + 1].to_broadcast([P, P]),
-                    rhs=bias_rows[:],
-                    start=True,
-                    stop=True,
-                )
+                for u in range(2):
+                    nc.tensor.transpose(
+                        spread[:, i, u, :],
+                        bias_cols[:, u, c + i : c + i + 1].to_broadcast([P, P]),
+                        ident_f32[:],
+                    )
             if c < GROUPS:
                 dst = b1_all[:, c : c + 2, :].bitcast(F32).rearrange("p i (u q) -> p i u q", u=2)
-                src = spread[:].bitcast(F32).rearrange("p i (q u) -> p i u q", u=2)
-            else:
-                dst = tail_bias[:]
                 src = spread[:]
+            else:
+                dst = tail_bias[:].bitcast(F32).rearrange("p i (q u) -> p i q u", u=2)
+                src = spread[:].rearrange("p i u q -> p i q u")
             if c % 4 == 0:
                 nc.vector.tensor_copy(out=dst, in_=src)
             else:
                 nc.scalar.copy(out=dst, in_=src)
 
         h_tiles = {}
-        flipped_tiles = {}
         grouped_tiles = {}
         h_codes = {}
         h_planes = {}
@@ -184,10 +195,12 @@ def tile_selectivemixing_pa_k_kernel(
                 h_tiles[g] = h
 
         def flip_round(r):
+            flipped_tiles = {}
             for g in range(ROUND * r, ROUND * (r + 1)):
                 flipped_tiles[g] = flip(h_tiles[g][:].bitcast(F32).rearrange("p t (u q) -> p t u q", u=2))
             for g in range(ROUND * r, ROUND * (r + 1)):
-                grouped_tiles[g] = regroup(flipped_tiles[g])
+                copy = nc.vector.tensor_copy if g % 4 == 3 else nc.scalar.copy
+                grouped_tiles[g] = regroup(flipped_tiles[g], copy)
 
         def quantise_round(r):
             for g in range(ROUND * r, ROUND * (r + 1)):
@@ -230,13 +243,14 @@ def tile_selectivemixing_pa_k_kernel(
             if r < ROUNDS:
                 first_layer(r)
             if r == ROUNDS:
+                nc.scalar.activation(out=warm[:], in_=zero[:], func=ACT.Sigmoid)
                 value_path()
             if r >= LAG:
                 second_layer(r - LAG)
-            if 1 <= r <= ROUNDS:
-                flip_round(r - 1)
             if 2 <= r <= ROUNDS + 1:
                 quantise_round(r - 2)
+            if 1 <= r <= ROUNDS:
+                flip_round(r - 1)
 
         for t in range(TOKEN_TILES):
             gate = work.tile([P, D], F32, bufs=2)

@@ -14,17 +14,16 @@ ADD = mybir.AluOpType.add
 MULT = mybir.AluOpType.mult
 
 P = 128
+PACK = 4
 TOKENS = 256
 TOKEN_TILES = TOKENS // P
 D = 512
 F = 16384
 GROUPS = F // D
-ROUND = 2
-ROUNDS = GROUPS // ROUND
-LAG = 3
-WEIGHT_BUFS = 8
-QUARTER = F // 4
-BIAS_ROWS = GROUPS + 2
+QUARTERS = 4
+CHUNKS = GROUPS // QUARTERS
+W1_AHEAD = 3
+SECOND_START = 7
 
 FLOPS = 2 * TOKENS * (D * F + F * D + D * D)
 
@@ -35,25 +34,26 @@ def tile_selectivemixing_pa_k_kernel(
     nc = tc.nc
     x_rows = x.flatten_outer_dims()
     out_rows = out.flatten_outer_dims()
-    w1_dram = W1_words[0].rearrange("p n t -> p (n t)").bitcast(I32)
+    w1_dram = W1_words[0].rearrange("p n t -> p (n t)").bitcast(I32).rearrange("p (j a n) -> p j a n", j=QUARTERS, a=CHUNKS)
+    w2_dram = W2g_words.rearrange("(j a) p n t -> a p j (n t)", j=QUARTERS)
 
     with ExitStack() as stack:
         consts = stack.enter_context(tc.tile_pool(name="consts", bufs=1))
-        weights = stack.enter_context(tc.tile_pool(name="weights", bufs=WEIGHT_BUFS))
-        work = stack.enter_context(tc.tile_pool(name="work", bufs=4))
+        weights = stack.enter_context(tc.tile_pool(name="weights", bufs=CHUNKS))
+        work = stack.enter_context(tc.tile_pool(name="work", bufs=3))
         psum_acc = stack.enter_context(tc.psum_pool(name="psum_acc", bufs=1))
-        psum_z = stack.enter_context(tc.psum_pool(name="psum_z", bufs=2 * ROUND))
-        psum_flip = stack.enter_context(tc.psum_pool(name="psum_flip", bufs=ROUND))
+        psum_z = stack.enter_context(tc.psum_pool(name="psum_z", bufs=6))
         stack.enter_context(tc.manual_schedule())
 
-        w1_planes = consts.tile([P, QUARTER], U8, align_bytes=64)
+        w1_planes_raw = consts.tile([P, CHUNKS, P, PACK], U8, align_bytes=64)
+        w1_planes = consts.tile([P, CHUNKS, PACK, P], U8, align_bytes=64)
         bias_rows = consts.tile([P, D], BF16)
-        w2_planes = consts.tile([P, GROUPS, D], U8, align_bytes=64)
+        w2_planes = consts.tile([P, CHUNKS, D], U8, align_bytes=64)
         wv_plane = consts.tile([P, D], U8, align_bytes=64)
         zero = consts.tile([P, 1], F32)
         warm = consts.tile([P, 1], F32)
+        nc.vector.memset(w1_planes_raw[:].rearrange("p a m t -> p (a m t)").bitcast(I32), 0)
         nc.vector.memset(zero[:], 0.0)
-        nc.vector.memset(w1_planes[:].bitcast(I32), 0)
         nc.vector.memset(bias_rows[:].bitcast(I32), 0)
         nc.vector.memset(w2_planes[:].bitcast(I32), 0)
         nc.vector.memset(wv_plane[:].bitcast(I32), 0)
@@ -61,74 +61,72 @@ def tile_selectivemixing_pa_k_kernel(
         ident_f32 = consts.tile([P, P], F32)
         make_identity(nc, ident_f32[:])
 
+        x_sb = consts.tile([P, TOKEN_TILES, D], BF16)
+        nc.scalar.dma_start(out=x_sb[:], in_=x_rows.rearrange("(t p) d -> p t d", p=P))
         nc.scalar.dma_start(out=bias_rows[0:GROUPS, :], in_=b1.rearrange("(g n) -> g n", n=D))
         nc.scalar.dma_start(out=bias_rows[GROUPS : GROUPS + 1, :], in_=b2g.rearrange("(o n) -> o n", o=1))
         nc.scalar.dma_start(out=bias_rows[GROUPS + 1 : GROUPS + 2, :], in_=bv.rearrange("(o n) -> o n", o=1))
         nc.scalar.activation(out=warm[:], in_=zero[:], func=ACT.Silu)
-        x_sb = consts.tile([P, TOKEN_TILES, D], BF16)
-        nc.sync.dma_start(out=x_sb[:], in_=x_rows.rearrange("(t p) d -> p t d", p=P))
-        w1_scale_quarters = W1_scales[0].bitcast(I32).rearrange("q (k n) -> k q n", k=4)
+
+        w1_scale_quarters = W1_scales[0].bitcast(I32).rearrange("q (j n) -> j q n", j=QUARTERS)
         for quadrant in range(4):
             nc.sync.dma_start(
-                out=w1_planes[32 * quadrant : 32 * quadrant + 16, :].bitcast(I32),
+                out=w1_planes_raw[32 * quadrant : 32 * quadrant + 16].rearrange("p a m t -> p (a m t)").bitcast(I32),
                 in_=w1_scale_quarters[:, 4 * quadrant : 4 * quadrant + 4, :],
             )
 
         w1_tiles = {}
         w2_tiles = {}
 
-        def load_w1(r):
-            w1 = weights.tile([P, ROUND * D], U32, align_bytes=64)
-            nc.sync.dma_start(out=w1[:].bitcast(I32), in_=w1_dram[:, ROUND * D * r : ROUND * D * (r + 1)])
-            w1_tiles[r] = w1
+        def load_w1(a, pieces):
+            w1 = weights.tile([P, QUARTERS, D], U32, align_bytes=64)
+            step = QUARTERS // pieces
+            for j in range(0, QUARTERS, step):
+                nc.sync.dma_start(out=w1[:, j : j + step, :].bitcast(I32), in_=w1_dram[:, j : j + step, a, :])
+            w1_tiles[a] = w1
 
-        def load_w2(r):
-            w2 = weights.tile([P, ROUND, D], U32, align_bytes=64)
-            nc.sync.dma_start(
-                out=w2[:].bitcast(I32),
-                in_=W2g_words[ROUND * r : ROUND * (r + 1)].rearrange("g p n t -> p g (n t)").bitcast(I32),
-            )
-            w2_tiles[r] = w2
+        def load_w2(a):
+            w2 = weights.tile([P, QUARTERS, D], U32, align_bytes=64)
+            nc.sync.dma_start(out=w2[:].bitcast(I32), in_=w2_dram[a].bitcast(I32))
+            w2_tiles[a] = w2
 
-        for r in range(LAG):
-            load_w1(r)
+        load_w1(0, QUARTERS)
+        for a in range(1, W1_AHEAD):
+            load_w1(a, 1)
         for quadrant in range(4):
-            nc.sync.dma_start(
-                out=w2_planes[32 * quadrant : 32 * quadrant + 4, :, :].bitcast(I32),
-                in_=W2g_scales[:, 4 * quadrant : 4 * quadrant + 4, :].bitcast(I32).rearrange("g r n -> r g n"),
-            )
-        for r in range(ROUNDS):
-            load_w2(r)
-            if r + LAG < ROUNDS:
-                load_w1(r + LAG)
-        wv_words = consts.tile([P, D], U32, align_bytes=64)
-        nc.sync.dma_start(out=wv_words[:].bitcast(I32), in_=Wv_words[0].rearrange("p n t -> p (n t)").bitcast(I32))
+            for j in range(QUARTERS):
+                row = 32 * quadrant + 4 * j
+                nc.sync.dma_start(
+                    out=w2_planes[row : row + 4, :, :].bitcast(I32),
+                    in_=W2g_scales[CHUNKS * j : CHUNKS * (j + 1), 4 * quadrant : 4 * quadrant + 4, :]
+                    .bitcast(I32)
+                    .rearrange("a r n -> r a n"),
+                )
         for quadrant in range(4):
             nc.sync.dma_start(
                 out=wv_plane[32 * quadrant : 32 * quadrant + 4, :].bitcast(I32),
                 in_=Wv_scales[0][4 * quadrant : 4 * quadrant + 4, :].bitcast(I32),
             )
+        wv_words = consts.tile([P, D], U32, align_bytes=64)
+        nc.sync.dma_start(out=wv_words[:].bitcast(I32), in_=Wv_words[0].rearrange("p n t -> p (n t)").bitcast(I32))
+        for a in range(CHUNKS):
+            load_w2(a)
+            if a + W1_AHEAD < CHUNKS:
+                load_w1(a + W1_AHEAD, 1)
 
-        def flip(words):
-            flipped = psum_flip.tile([P, TOKEN_TILES, 2, P], F32, tag="flip")
-            for t in range(TOKEN_TILES):
-                for u in range(2):
-                    nc.tensor.transpose(flipped[:, t, u, :], words[:, t, u, :], ident_f32[:])
-            return flipped
-
-        def regroup(flipped, copy):
-            grouped = work.tile([P, TOKENS * 4], BF16, align_bytes=64)
-            copy(
-                out=grouped[:].bitcast(F32).rearrange("p (t k u) -> p t k u", t=TOKEN_TILES, u=2),
-                in_=flipped[:].rearrange("p t u k -> p t k u"),
-            )
-            return grouped
-
-        def quantise(grouped, codes, plane):
-            nc.vector.quantize_mx(out=codes[:].bitcast(FP8X4), scales=plane[:], in_=grouped[:])
+        x_words = x_sb[:].bitcast(F32).rearrange("p t (q u) -> p t u q", u=2)
+        x_flipped = psum_z.tile([P, TOKEN_TILES, 2, P], F32, tag="z")
+        for t in range(TOKEN_TILES):
+            for u in range(2):
+                nc.tensor.transpose(x_flipped[:, t, u, :], x_words[:, t, u, :], ident_f32[:])
+        x_grouped = consts.tile([P, TOKENS * PACK], BF16, align_bytes=64)
+        nc.vector.tensor_copy(
+            out=x_grouped[:].bitcast(F32).rearrange("p (t k u) -> p t k u", t=TOKEN_TILES, u=2),
+            in_=x_flipped[:].rearrange("p t u k -> p t k u"),
+        )
 
         bias_words = bias_rows[:].bitcast(F32).rearrange("c (q u) -> c u q", u=2)
-        bias_flipped = psum_flip.tile([P, 2, P], F32, tag="flip")
+        bias_flipped = psum_z.tile([P, 2, P], F32, tag="z")
         for u in range(2):
             nc.tensor.transpose(bias_flipped[:, u, :], bias_words[:, u, :], ident_f32[:])
         bias_cols = consts.tile([P, 2, P], F32)
@@ -136,121 +134,144 @@ def tile_selectivemixing_pa_k_kernel(
 
         x_codes = consts.tile([P, TOKENS], U32, align_bytes=64)
         x_plane = consts.tile([P, TOKENS], U8, align_bytes=64)
-        x_flipped = flip(x_sb[:].bitcast(F32).rearrange("p t (q u) -> p t u q", u=2))
-        x_grouped = regroup(x_flipped, nc.vector.tensor_copy)
-        quantise(x_grouped, x_codes, x_plane)
+        nc.vector.quantize_mx(out=x_codes[:].bitcast(FP8X4), scales=x_plane[:], in_=x_grouped[:])
 
-        b1_all = consts.tile([P, GROUPS, D], BF16)
+        b1_cols = consts.tile([P, GROUPS, PACK], F32)
+        nc.vector.tensor_copy(
+            out=b1_cols[:].rearrange("p c (u e) -> p c u e", u=2),
+            in_=bias_cols[:].bitcast(BF16).rearrange("p u (c e) -> p c u e", e=2)[:, 0:GROUPS],
+        )
+
         tail_bias = consts.tile([P, 2, D], BF16)
-        for c in range(0, BIAS_ROWS, 2):
-            spread = psum_z.tile([P, 2, 2, P], F32, tag="z")
-            for i in range(2):
-                for u in range(2):
-                    nc.tensor.transpose(
-                        spread[:, i, u, :],
-                        bias_cols[:, u, c + i : c + i + 1].to_broadcast([P, P]),
-                        ident_f32[:],
-                    )
-            if c < GROUPS:
-                dst = b1_all[:, c : c + 2, :].bitcast(F32).rearrange("p i (u q) -> p i u q", u=2)
-                src = spread[:]
-            else:
-                dst = tail_bias[:].bitcast(F32).rearrange("p i (q u) -> p i q u", u=2)
-                src = spread[:].rearrange("p i u q -> p i q u")
-            if c % 4 == 0:
-                nc.vector.tensor_copy(out=dst, in_=src)
-            else:
-                nc.scalar.copy(out=dst, in_=src)
+        spread = psum_z.tile([P, 2, 2, P], F32, tag="z")
+        for i in range(2):
+            for u in range(2):
+                nc.tensor.transpose(
+                    spread[:, i, u, :],
+                    bias_cols[:, u, GROUPS + i : GROUPS + i + 1].to_broadcast([P, P]),
+                    ident_f32[:],
+                )
+        nc.scalar.copy(
+            out=tail_bias[:].bitcast(F32).rearrange("p i (q u) -> p i q u", u=2),
+            in_=spread[:].rearrange("p i u q -> p i q u"),
+        )
 
+        w1_sorted = {}
+        z_tiles = {}
         h_tiles = {}
         grouped_tiles = {}
         h_codes = {}
         h_planes = {}
         acc = [psum_acc.tile([P, D], F32, name="acc%d" % t) for t in range(TOKEN_TILES)]
 
-        def first_layer(r):
-            for g in range(ROUND * r, ROUND * (r + 1)):
-                offset = 4 * (g * D // QUARTER)
-                cols = g * D % QUARTER
-                zb = work.tile([P, TOKEN_TILES, D], F32)
-                for t in range(TOKEN_TILES):
-                    z = psum_z.tile([P, D], F32, tag="z")
+        def sort_planes(a):
+            nc.vector.tensor_copy(out=w1_planes[:, a, :, :], in_=w1_planes_raw[:, a, :, :].rearrange("p m t -> p t m"))
+
+        def sort_codes(i):
+            a, j = i // QUARTERS, i % QUARTERS
+            w1s = work.tile([P, D], U32, align_bytes=64, bufs=4)
+            nc.vector.tensor_copy(
+                out=w1s[:].bitcast(I32).rearrange("p (t m) -> p t m", t=PACK),
+                in_=w1_tiles[a][:, j, :].bitcast(I32).rearrange("p (m t) -> p t m", t=PACK),
+            )
+            w1_sorted[i] = w1s
+
+        def first_layer(i):
+            a, j = i // QUARTERS, i % QUARTERS
+            for half in range(2):
+                z = psum_z.tile([P, 2, TOKENS], F32, tag="z")
+                for s in range(2):
+                    t = 2 * half + s
                     nc.tensor.matmul_mx(
-                        out=z[:],
-                        lhsT=x_codes[:, P * t : P * (t + 1)].bitcast(FP8X4),
-                        lhsT_scale=x_plane[:, P * t : P * (t + 1)],
-                        rhs=w1_tiles[r][:, D * (g % ROUND) : D * (g % ROUND + 1)].bitcast(FP8X4),
-                        rhs_scale=w1_planes[offset:P, cols : cols + D],
+                        out=z[:, s, :],
+                        lhsT=w1_sorted[i][:, P * t : P * (t + 1)].bitcast(FP8X4),
+                        lhsT_scale=w1_planes[4 * j : P, a, t, :],
+                        rhs=x_codes[:].bitcast(FP8X4),
+                        rhs_scale=x_plane[:],
                         start=True,
                         stop=True,
                     )
-                    nc.vector.tensor_tensor(
-                        out=zb[:, t, :].rearrange("p (u q e) -> p u q e", u=2, e=2),
-                        in0=z[:].rearrange("p (q u e) -> p u q e", u=2, e=2),
-                        in1=b1_all[:, g, :].rearrange("p (u q e) -> p u q e", u=2, e=2),
-                        op=ADD,
-                    )
-                h = work.tile([P, TOKEN_TILES, D], BF16, bufs=6)
-                nc.scalar.activation(out=h[:], in_=zb[:], func=ACT.Silu)
-                h_tiles[g] = h
+                z_tiles[(i, half)] = z
 
-        def flip_round(r):
-            flipped_tiles = {}
-            for g in range(ROUND * r, ROUND * (r + 1)):
-                flipped_tiles[g] = flip(h_tiles[g][:].bitcast(F32).rearrange("p t (u q) -> p t u q", u=2))
-            for g in range(ROUND * r, ROUND * (r + 1)):
-                copy = nc.vector.tensor_copy if g % 4 == 3 else nc.scalar.copy
-                grouped_tiles[g] = regroup(flipped_tiles[g], copy)
+        def silu(i):
+            g = CHUNKS * (i % QUARTERS) + i // QUARTERS
+            h = work.tile([P, PACK, TOKENS], BF16)
+            for t in range(PACK):
+                nc.scalar.activation(
+                    out=h[:, t, :], in_=z_tiles[(i, t // 2)][:, t % 2, :], func=ACT.Silu, bias=b1_cols[:, g, t : t + 1]
+                )
+            h_tiles[i] = h
 
-        def quantise_round(r):
-            for g in range(ROUND * r, ROUND * (r + 1)):
-                codes = work.tile([P, TOKENS], U32, align_bytes=64, bufs=6)
-                plane = work.tile([P, TOKENS], U8, align_bytes=64, bufs=6)
-                quantise(grouped_tiles[g], codes, plane)
-                h_codes[g] = codes
-                h_planes[g] = plane
+        def interleave(i):
+            grouped = work.tile([P, TOKENS * PACK], BF16, align_bytes=64)
+            nc.vector.tensor_copy(
+                out=grouped[:].rearrange("p (n t) -> p n t", t=PACK), in_=h_tiles[i][:].rearrange("p t n -> p n t")
+            )
+            grouped_tiles[i] = grouped
 
-        def second_layer(r):
-            for g in range(ROUND * r, ROUND * (r + 1)):
-                for t in range(TOKEN_TILES):
-                    nc.tensor.matmul_mx(
-                        out=acc[t][:],
-                        lhsT=h_codes[g][:, P * t : P * (t + 1)].bitcast(FP8X4),
-                        lhsT_scale=h_planes[g][:, P * t : P * (t + 1)],
-                        rhs=w2_tiles[r][:, g % ROUND, :].bitcast(FP8X4),
-                        rhs_scale=w2_planes[:, g, :],
-                        start=(g == 0),
-                        stop=(g == GROUPS - 1),
-                    )
+        def quantise(i):
+            codes = work.tile([P, TOKENS], U32, align_bytes=64, bufs=12)
+            plane = work.tile([P, TOKENS], U8, align_bytes=64, bufs=12)
+            nc.vector.quantize_mx(out=codes[:].bitcast(FP8X4), scales=plane[:], in_=grouped_tiles[i][:])
+            h_codes[i] = codes
+            h_planes[i] = plane
+
+        def second_layer(i):
+            a, j = i // QUARTERS, i % QUARTERS
+            for t in range(TOKEN_TILES):
+                nc.tensor.matmul_mx(
+                    out=acc[t][:],
+                    lhsT=h_codes[i][:, P * t : P * (t + 1)].bitcast(FP8X4),
+                    lhsT_scale=h_planes[i][:, P * t : P * (t + 1)],
+                    rhs=w2_tiles[a][:, j, :].bitcast(FP8X4),
+                    rhs_scale=w2_planes[4 * j : P, a, :],
+                    start=(i == 0),
+                    stop=(i == GROUPS - 1),
+                )
 
         values = consts.tile([P, TOKEN_TILES, D], F32)
+        v_tiles = {}
 
-        def value_path():
-            for t in range(TOKEN_TILES):
-                v = psum_z.tile([P, D], F32, tag="z")
-                nc.tensor.matmul_mx(
-                    out=v[:],
-                    lhsT=x_codes[:, P * t : P * (t + 1)].bitcast(FP8X4),
-                    lhsT_scale=x_plane[:, P * t : P * (t + 1)],
-                    rhs=wv_words[:].bitcast(FP8X4),
-                    rhs_scale=wv_plane[:],
-                    start=True,
-                    stop=True,
-                )
-                nc.vector.tensor_tensor(out=values[:, t, :], in0=v[:], in1=tail_bias[:, 1, :], op=ADD)
+        def value_product(t):
+            v = psum_z.tile([P, D], F32, tag="z")
+            nc.tensor.matmul_mx(
+                out=v[:],
+                lhsT=x_codes[:, P * t : P * (t + 1)].bitcast(FP8X4),
+                lhsT_scale=x_plane[:, P * t : P * (t + 1)],
+                rhs=wv_words[:].bitcast(FP8X4),
+                rhs_scale=wv_plane[:],
+                start=True,
+                stop=True,
+            )
+            v_tiles[t] = v
 
-        for r in range(ROUNDS + LAG):
-            if r < ROUNDS:
-                first_layer(r)
-            if r == ROUNDS:
+        def value_bias(t):
+            nc.vector.tensor_tensor(out=values[:, t, :], in0=v_tiles[t][:], in1=tail_bias[:, 1, :], op=ADD)
+
+        seconds = 0
+        for s in range(-3, GROUPS + 1):
+            if 1 <= s <= GROUPS:
+                interleave(s - 1)
+            if s + 3 < GROUPS:
+                if (s + 3) % QUARTERS == 0:
+                    sort_planes((s + 3) // QUARTERS)
+                sort_codes(s + 3)
+            elif s >= GROUPS - 1:
+                value_bias(s - (GROUPS - 1))
+            if 1 <= s <= GROUPS:
+                quantise(s - 1)
+            if 0 <= s + 2 < GROUPS:
+                first_layer(s + 2)
+            elif s + 2 == GROUPS:
+                for t in range(TOKEN_TILES):
+                    value_product(t)
+            while seconds <= s - 1 and (s == GROUPS or 4 * seconds <= 5 * (s - SECOND_START)):
+                second_layer(seconds)
+                seconds += 1
+            if 0 <= s < GROUPS:
+                silu(s)
+            if s == GROUPS:
                 nc.scalar.activation(out=warm[:], in_=zero[:], func=ACT.Sigmoid)
-                value_path()
-            if r >= LAG:
-                second_layer(r - LAG)
-            if 2 <= r <= ROUNDS + 1:
-                quantise_round(r - 2)
-            if 1 <= r <= ROUNDS:
-                flip_round(r - 1)
 
         for t in range(TOKEN_TILES):
             gate = work.tile([P, D], F32, bufs=2)

@@ -171,8 +171,8 @@ def tile_selectivemixing_pa_k_kernel(
             a, j = i // QUARTERS, i % QUARTERS
             w1s = work.tile([P, D], U32, align_bytes=64, bufs=4)
             nc.vector.tensor_copy(
-                out=w1s[:].bitcast(I32).rearrange("p (t m) -> p t m", t=PACK),
-                in_=w1_tiles[a][:, j, :].bitcast(I32).rearrange("p (m t) -> p t m", t=PACK),
+                out=w1s[:].bitcast(I32).rearrange("p (t m) -> p m t", t=PACK),
+                in_=w1_tiles[a][:, j, :].bitcast(I32).rearrange("p (m t) -> p m t", t=PACK),
             )
             w1_sorted[i] = w1s
 

@@ -85,7 +85,14 @@ def tile_selectivemixing_pa_k_kernel(
                 nc.sync.dma_start(out=w1[:, j : j + step, :].bitcast(I32), in_=w1_dram[:, j : j + step, a, :])
             w1_tiles[a] = w1
 
+        w2_scale_chunks = W2g_scales.bitcast(I32).rearrange("(j a) q n -> a j q n", j=QUARTERS)
+
         def load_w2(a):
+            for quadrant in range(4):
+                nc.sync.dma_start(
+                    out=w2_planes[32 * quadrant : 32 * quadrant + 16, a, :].bitcast(I32),
+                    in_=w2_scale_chunks[a][:, 4 * quadrant : 4 * quadrant + 4, :],
+                )
             w2 = weights.tile([P, QUARTERS, D], U32, align_bytes=64)
             nc.sync.dma_start(out=w2[:].bitcast(I32), in_=w2_dram[a].bitcast(I32))
             w2_tiles[a] = w2
@@ -93,26 +100,20 @@ def tile_selectivemixing_pa_k_kernel(
         load_w1(0, QUARTERS)
         for a in range(1, W1_AHEAD):
             load_w1(a, 1)
-        for quadrant in range(4):
-            for j in range(QUARTERS):
-                row = 32 * quadrant + 4 * j
-                nc.sync.dma_start(
-                    out=w2_planes[row : row + 4, :, :].bitcast(I32),
-                    in_=W2g_scales[CHUNKS * j : CHUNKS * (j + 1), 4 * quadrant : 4 * quadrant + 4, :]
-                    .bitcast(I32)
-                    .rearrange("a r n -> r a n"),
-                )
-        for quadrant in range(4):
-            nc.sync.dma_start(
-                out=wv_plane[32 * quadrant : 32 * quadrant + 4, :].bitcast(I32),
-                in_=Wv_scales[0][4 * quadrant : 4 * quadrant + 4, :].bitcast(I32),
-            )
         wv_words = consts.tile([P, D], U32, align_bytes=64)
-        nc.sync.dma_start(out=wv_words[:].bitcast(I32), in_=Wv_words[0].rearrange("p n t -> p (n t)").bitcast(I32))
         for a in range(CHUNKS):
             load_w2(a)
             if a + W1_AHEAD < CHUNKS:
                 load_w1(a + W1_AHEAD, 1)
+            if a + W1_AHEAD == CHUNKS:
+                for quadrant in range(4):
+                    nc.sync.dma_start(
+                        out=wv_plane[32 * quadrant : 32 * quadrant + 4, :].bitcast(I32),
+                        in_=Wv_scales[0][4 * quadrant : 4 * quadrant + 4, :].bitcast(I32),
+                    )
+                nc.sync.dma_start(
+                    out=wv_words[:].bitcast(I32), in_=Wv_words[0].rearrange("p n t -> p (n t)").bitcast(I32)
+                )
 
         x_words = x_sb[:].bitcast(F32).rearrange("p t (q u) -> p t u q", u=2)
         x_flipped = psum_z.tile([P, TOKEN_TILES, 2, P], F32, tag="z")

@@ -52,9 +52,10 @@ def tile_selectivemixing_pa_k_kernel(
         wv_plane = consts.tile([P, D], U8, align_bytes=64)
         zero = consts.tile([P, 1], F32)
         warm = consts.tile([P, 1], F32)
-        nc.vector.memset(w1_planes_raw[:].rearrange("p a m t -> p (a m t)").bitcast(I32), 0)
+        nc.vector.memset(w1_planes_raw[:, 0].rearrange("p m t -> p (m t)").bitcast(I32), 0)
         nc.vector.memset(zero[:], 0.0)
         nc.vector.memset(bias_rows[:].bitcast(I32), 0)
+        nc.vector.memset(w1_planes_raw[:, 1:CHUNKS].rearrange("p a m t -> p (a m t)").bitcast(I32), 0)
         nc.vector.memset(w2_planes[:].bitcast(I32), 0)
         nc.vector.memset(wv_plane[:].bitcast(I32), 0)
 
@@ -69,11 +70,6 @@ def tile_selectivemixing_pa_k_kernel(
         nc.scalar.activation(out=warm[:], in_=zero[:], func=ACT.Silu)
 
         w1_scale_quarters = W1_scales[0].bitcast(I32).rearrange("q (j n) -> j q n", j=QUARTERS)
-        for quadrant in range(4):
-            nc.sync.dma_start(
-                out=w1_planes_raw[32 * quadrant : 32 * quadrant + 16].rearrange("p a m t -> p (a m t)").bitcast(I32),
-                in_=w1_scale_quarters[:, 4 * quadrant : 4 * quadrant + 4, :],
-            )
 
         w1_tiles = {}
         w2_tiles = {}
@@ -83,7 +79,20 @@ def tile_selectivemixing_pa_k_kernel(
             step = QUARTERS // pieces
             for j in range(0, QUARTERS, step):
                 nc.sync.dma_start(out=w1[:, j : j + step, :].bitcast(I32), in_=w1_dram[:, j : j + step, a, :])
+                if a == 0 and j == 0:
+                    load_w1_scales(0, 1)
+            if a == 0:
+                load_w1_scales(1, CHUNKS)
             w1_tiles[a] = w1
+
+        def load_w1_scales(a0, a1):
+            for quadrant in range(4):
+                nc.sync.dma_start(
+                    out=w1_planes_raw[32 * quadrant : 32 * quadrant + 16, a0:a1]
+                    .rearrange("p a m t -> p (a m t)")
+                    .bitcast(I32),
+                    in_=w1_scale_quarters[:, 4 * quadrant : 4 * quadrant + 4, P * a0 : P * a1],
+                )
 
         w2_scale_chunks = W2g_scales.bitcast(I32).rearrange("(j a) q n -> a j q n", j=QUARTERS)
 
@@ -135,13 +144,7 @@ def tile_selectivemixing_pa_k_kernel(
 
         x_codes = consts.tile([P, TOKENS], U32, align_bytes=64)
         x_plane = consts.tile([P, TOKENS], U8, align_bytes=64)
-        nc.vector.quantize_mx(out=x_codes[:].bitcast(FP8X4), scales=x_plane[:], in_=x_grouped[:])
-
         b1_cols = consts.tile([P, GROUPS, PACK], F32)
-        nc.vector.tensor_copy(
-            out=b1_cols[:].rearrange("p c (u e) -> p c u e", u=2),
-            in_=bias_cols[:].bitcast(BF16).rearrange("p u (c e) -> p c u e", e=2)[:, 0:GROUPS],
-        )
 
         tail_bias = consts.tile([P, 2, D], BF16)
         spread = psum_z.tile([P, 2, 2, P], F32, tag="z")
@@ -197,29 +200,42 @@ def tile_selectivemixing_pa_k_kernel(
         def silu(i):
             g = CHUNKS * (i % QUARTERS) + i // QUARTERS
             h = work.tile([P, PACK, TOKENS], BF16)
-            for t in range(PACK):
-                nc.scalar.activation(
-                    out=h[:, t, :], in_=z_tiles[(i, t // 2)][:, t % 2, :], func=ACT.Silu, bias=b1_cols[:, g, t : t + 1]
-                )
+            pieces = TOKEN_TILES if i == GROUPS - 1 else 1
+            width = TOKENS // pieces
+            for n0 in range(0, TOKENS, width):
+                for t in range(PACK):
+                    nc.scalar.activation(
+                        out=h[:, t, n0 : n0 + width],
+                        in_=z_tiles[(i, t // 2)][:, t % 2, n0 : n0 + width],
+                        func=ACT.Silu,
+                        bias=b1_cols[:, g, t : t + 1],
+                    )
             h_tiles[i] = h
 
-        def interleave(i):
+        def new_tiles(i):
             grouped = work.tile([P, TOKENS * PACK], BF16, align_bytes=64)
-            nc.vector.tensor_copy(
-                out=grouped[:].rearrange("p (n t) -> p n t", t=PACK), in_=h_tiles[i][:].rearrange("p t n -> p n t")
-            )
-            grouped_tiles[i] = grouped
-
-        def quantise(i):
             codes = work.tile([P, TOKENS], U32, align_bytes=64, bufs=12)
             plane = work.tile([P, TOKENS], U8, align_bytes=64, bufs=12)
-            nc.vector.quantize_mx(out=codes[:].bitcast(FP8X4), scales=plane[:], in_=grouped_tiles[i][:])
+            grouped_tiles[i] = grouped
             h_codes[i] = codes
             h_planes[i] = plane
 
-        def second_layer(i):
+        def interleave(i, n0=0, width=TOKENS):
+            nc.vector.tensor_copy(
+                out=grouped_tiles[i][:, PACK * n0 : PACK * (n0 + width)].rearrange("p (n t) -> p n t", t=PACK),
+                in_=h_tiles[i][:, :, n0 : n0 + width].rearrange("p t n -> p n t"),
+            )
+
+        def quantise(i, n0=0, width=TOKENS):
+            nc.vector.quantize_mx(
+                out=h_codes[i][:, n0 : n0 + width].bitcast(FP8X4),
+                scales=h_planes[i][:, n0 : n0 + width],
+                in_=grouped_tiles[i][:, PACK * n0 : PACK * (n0 + width)],
+            )
+
+        def second_layer(i, tiles=(0, 1)):
             a, j = i // QUARTERS, i % QUARTERS
-            for t in range(TOKEN_TILES):
+            for t in tiles:
                 nc.tensor.matmul_mx(
                     out=acc[t][:],
                     lhsT=h_codes[i][:, P * t : P * (t + 1)].bitcast(FP8X4),
@@ -250,35 +266,57 @@ def tile_selectivemixing_pa_k_kernel(
             nc.vector.tensor_tensor(out=values[:, t, :], in0=v_tiles[t][:], in1=tail_bias[:, 1, :], op=ADD)
 
         seconds = 0
-        for s in range(-3, GROUPS + 1):
-            if 1 <= s <= GROUPS:
+        for s in range(-3, GROUPS):
+            if s >= 1:
+                new_tiles(s - 1)
                 interleave(s - 1)
             if s + 3 < GROUPS:
                 if (s + 3) % QUARTERS == 0:
                     sort_planes((s + 3) // QUARTERS)
+                if s + 3 == 0:
+                    nc.vector.quantize_mx(out=x_codes[:].bitcast(FP8X4), scales=x_plane[:], in_=x_grouped[:])
                 sort_codes(s + 3)
-            elif s >= GROUPS - 1:
-                value_bias(s - (GROUPS - 1))
-            if 1 <= s <= GROUPS:
+                if s + 3 == 0:
+                    nc.vector.tensor_copy(
+                        out=b1_cols[:].rearrange("p c (u e) -> p c u e", u=2),
+                        in_=bias_cols[:].bitcast(BF16).rearrange("p u (c e) -> p c u e", e=2)[:, 0:GROUPS],
+                    )
+            elif s >= GROUPS - 2:
+                value_bias(s - (GROUPS - 2))
+            if s >= 1:
                 quantise(s - 1)
-            if 0 <= s + 2 < GROUPS:
+            if 0 <= s + 2 < GROUPS - 1:
                 first_layer(s + 2)
-            elif s + 2 == GROUPS:
+            elif s + 2 == GROUPS - 1:
                 for t in range(TOKEN_TILES):
                     value_product(t)
-            while seconds <= s - 1 and (s == GROUPS or 4 * seconds <= 5 * (s - SECOND_START)):
+            elif s + 2 == GROUPS:
+                first_layer(GROUPS - 1)
+            while seconds <= s - 1 and 4 * seconds <= 5 * (s - SECOND_START):
                 second_layer(seconds)
                 seconds += 1
-            if 0 <= s < GROUPS:
+            if s >= 0:
                 silu(s)
-            if s == GROUPS:
-                nc.scalar.activation(out=warm[:], in_=zero[:], func=ACT.Sigmoid)
-
+        nc.scalar.activation(out=warm[:], in_=zero[:], func=ACT.Sigmoid)
+        while seconds < GROUPS - 1:
+            second_layer(seconds)
+            seconds += 1
+        new_tiles(GROUPS - 1)
         for t in range(TOKEN_TILES):
-            gate = work.tile([P, D], F32, bufs=2)
-            nc.vector.tensor_tensor(out=gate[:], in0=acc[t][:], in1=tail_bias[:, 0, :], op=ADD)
-            opened = work.tile([P, D], F32, bufs=2)
-            nc.scalar.activation(out=opened[:], in_=gate[:], func=ACT.Sigmoid)
-            result = work.tile([P, D], F32, bufs=2)
-            nc.vector.tensor_tensor(out=result[:], in0=values[:, t, :], in1=opened[:], op=MULT)
-            nc.sync.dma_start(out=out_rows[P * t : P * (t + 1), :], in_=result[:])
+            interleave(GROUPS - 1, P * t, P)
+            quantise(GROUPS - 1, P * t, P)
+            second_layer(GROUPS - 1, (t,))
+
+        gates = {}
+        half = D // 2
+        pieces = [(t, c) for t in range(TOKEN_TILES) for c in range(0, D, half)]
+        for t, c in pieces:
+            gate = work.tile([P, half], F32, bufs=4)
+            nc.vector.tensor_tensor(out=gate[:], in0=acc[t][:, c : c + half], in1=tail_bias[:, 0, c : c + half], op=ADD)
+            gates[(t, c)] = gate
+        for t, c in pieces:
+            opened = work.tile([P, half], F32, bufs=4)
+            nc.scalar.activation(out=opened[:], in_=gates[(t, c)][:], func=ACT.Sigmoid)
+            result = work.tile([P, half], F32, bufs=4)
+            nc.vector.tensor_tensor(out=result[:], in0=values[:, t, c : c + half], in1=opened[:], op=MULT)
+            nc.sync.dma_start(out=out_rows[P * t : P * (t + 1), c : c + half], in_=result[:])

@@ -24,6 +24,7 @@ QUARTERS = 4
 CHUNKS = GROUPS // QUARTERS
 W1_AHEAD = 3
 SECOND_START = 7
+SCALAR_EVERY = 10
 
 FLOPS = 2 * TOKENS * (D * F + F * D + D * D)
 
@@ -220,10 +221,14 @@ def tile_selectivemixing_pa_k_kernel(
             h_codes[i] = codes
             h_planes[i] = plane
 
+        def on_scalar(i):
+            return i >= 0 and i % SCALAR_EVERY == SCALAR_EVERY // 2
+
         def interleave(i, n0=0, width=TOKENS):
-            nc.vector.tensor_copy(
-                out=grouped_tiles[i][:, PACK * n0 : PACK * (n0 + width)].rearrange("p (n t) -> p n t", t=PACK),
-                in_=h_tiles[i][:, :, n0 : n0 + width].rearrange("p t n -> p n t"),
+            copy = nc.scalar.copy if on_scalar(i) else nc.vector.tensor_copy
+            copy(
+                out=grouped_tiles[i][:, PACK * n0 : PACK * (n0 + width)].rearrange("p (c i t) -> p c t i", i=4, t=PACK),
+                in_=h_tiles[i][:, :, n0 : n0 + width].rearrange("p t (c i) -> p c t i", i=4),
             )
 
         def quantise(i, n0=0, width=TOKENS):
@@ -266,8 +271,12 @@ def tile_selectivemixing_pa_k_kernel(
             nc.vector.tensor_tensor(out=values[:, t, :], in0=v_tiles[t][:], in1=tail_bias[:, 1, :], op=ADD)
 
         seconds = 0
+        quantised = 0
         for s in range(-3, GROUPS):
-            if s >= 1:
+            if on_scalar(s - 2):
+                quantise(s - 2)
+                quantised = s - 1
+            if s >= 1 and not on_scalar(s - 1):
                 new_tiles(s - 1)
                 interleave(s - 1)
             if s + 3 < GROUPS:
@@ -283,8 +292,9 @@ def tile_selectivemixing_pa_k_kernel(
                     )
             elif s >= GROUPS - 2:
                 value_bias(s - (GROUPS - 2))
-            if s >= 1:
+            if s >= 1 and not on_scalar(s - 1):
                 quantise(s - 1)
+                quantised = s
             if 0 <= s + 2 < GROUPS - 1:
                 first_layer(s + 2)
             elif s + 2 == GROUPS - 1:
@@ -292,11 +302,14 @@ def tile_selectivemixing_pa_k_kernel(
                     value_product(t)
             elif s + 2 == GROUPS:
                 first_layer(GROUPS - 1)
-            while seconds <= s - 1 and 4 * seconds <= 5 * (s - SECOND_START):
+            while seconds < quantised and 4 * seconds <= 5 * (s - SECOND_START):
                 second_layer(seconds)
                 seconds += 1
             if s >= 0:
                 silu(s)
+            if on_scalar(s - 1):
+                new_tiles(s - 1)
+                interleave(s - 1)
         nc.scalar.activation(out=warm[:], in_=zero[:], func=ACT.Sigmoid)
         while seconds < GROUPS - 1:
             second_layer(seconds)

@@ -24,7 +24,7 @@ QUARTERS = 4
 CHUNKS = GROUPS // QUARTERS
 W1_AHEAD = 3
 SECOND_START = 7
-SCALAR_EVERY = 10
+SCALAR_EVERY = 11
 
 FLOPS = 2 * TOKENS * (D * F + F * D + D * D)
 
@@ -222,7 +222,7 @@ def tile_selectivemixing_pa_k_kernel(
             h_planes[i] = plane
 
         def on_scalar(i):
-            return i >= 0 and i % SCALAR_EVERY == SCALAR_EVERY // 2
+            return i >= 0 and i % SCALAR_EVERY == SCALAR_EVERY - 1
 
         def interleave(i, n0=0, width=TOKENS):
             copy = nc.scalar.copy if on_scalar(i) else nc.vector.tensor_copy

@@ -23,6 +23,8 @@ GROUPS = F // D
 QUARTERS = 4
 CHUNKS = GROUPS // QUARTERS
 W1_AHEAD = 3
+HEAD_CHUNKS = 2
+WV_BEHIND = 3
 SECOND_START = 7
 SCALAR_EVERY = 11
 
@@ -49,14 +51,16 @@ def tile_selectivemixing_pa_k_kernel(
         w1_planes_raw = consts.tile([P, CHUNKS, P, PACK], U8, align_bytes=64)
         w1_planes = consts.tile([P, CHUNKS, PACK, P], U8, align_bytes=64)
         bias_rows = consts.tile([P, D], BF16)
+        tail_rows = consts.tile([P, D], BF16)
         w2_planes = consts.tile([P, CHUNKS, D], U8, align_bytes=64)
         wv_plane = consts.tile([P, D], U8, align_bytes=64)
         zero = consts.tile([P, 1], F32)
         warm = consts.tile([P, 1], F32)
-        nc.vector.memset(w1_planes_raw[:, 0].rearrange("p m t -> p (m t)").bitcast(I32), 0)
+        nc.vector.memset(w1_planes_raw[:, 0:HEAD_CHUNKS].rearrange("p a m t -> p (a m t)").bitcast(I32), 0)
         nc.vector.memset(zero[:], 0.0)
         nc.vector.memset(bias_rows[:].bitcast(I32), 0)
-        nc.vector.memset(w1_planes_raw[:, 1:CHUNKS].rearrange("p a m t -> p (a m t)").bitcast(I32), 0)
+        nc.vector.memset(tail_rows[:].bitcast(I32), 0)
+        nc.vector.memset(w1_planes_raw[:, HEAD_CHUNKS:CHUNKS].rearrange("p a m t -> p (a m t)").bitcast(I32), 0)
         nc.vector.memset(w2_planes[:].bitcast(I32), 0)
         nc.vector.memset(wv_plane[:].bitcast(I32), 0)
 
@@ -66,8 +70,6 @@ def tile_selectivemixing_pa_k_kernel(
         x_sb = consts.tile([P, TOKEN_TILES, D], BF16)
         nc.scalar.dma_start(out=x_sb[:], in_=x_rows.rearrange("(t p) d -> p t d", p=P))
         nc.scalar.dma_start(out=bias_rows[0:GROUPS, :], in_=b1.rearrange("(g n) -> g n", n=D))
-        nc.scalar.dma_start(out=bias_rows[GROUPS : GROUPS + 1, :], in_=b2g.rearrange("(o n) -> o n", o=1))
-        nc.scalar.dma_start(out=bias_rows[GROUPS + 1 : GROUPS + 2, :], in_=bv.rearrange("(o n) -> o n", o=1))
         nc.scalar.activation(out=warm[:], in_=zero[:], func=ACT.Silu)
 
         w1_scale_quarters = W1_scales[0].bitcast(I32).rearrange("q (j n) -> j q n", j=QUARTERS)
@@ -75,16 +77,10 @@ def tile_selectivemixing_pa_k_kernel(
         w1_tiles = {}
         w2_tiles = {}
 
-        def load_w1(a, pieces):
-            w1 = weights.tile([P, QUARTERS, D], U32, align_bytes=64)
-            step = QUARTERS // pieces
-            for j in range(0, QUARTERS, step):
-                nc.sync.dma_start(out=w1[:, j : j + step, :].bitcast(I32), in_=w1_dram[:, j : j + step, a, :])
-                if a == 0 and j == 0:
-                    load_w1_scales(0, 1)
-            if a == 0:
-                load_w1_scales(1, CHUNKS)
-            w1_tiles[a] = w1
+        def load_w1(a, j0=0, j1=QUARTERS):
+            if j0 == 0:
+                w1_tiles[a] = weights.tile([P, QUARTERS, D], U32, align_bytes=64, name="w1")
+            nc.sync.dma_start(out=w1_tiles[a][:, j0:j1, :].bitcast(I32), in_=w1_dram[:, j0:j1, a, :])
 
         def load_w1_scales(a0, a1):
             for quadrant in range(4):
@@ -97,30 +93,43 @@ def tile_selectivemixing_pa_k_kernel(
 
         w2_scale_chunks = W2g_scales.bitcast(I32).rearrange("(j a) q n -> a j q n", j=QUARTERS)
 
-        def load_w2(a):
+        def load_w2_scales(a):
             for quadrant in range(4):
                 nc.sync.dma_start(
                     out=w2_planes[32 * quadrant : 32 * quadrant + 16, a, :].bitcast(I32),
                     in_=w2_scale_chunks[a][:, 4 * quadrant : 4 * quadrant + 4, :],
                 )
+
+        def load_w2(a, pieces=1):
             w2 = weights.tile([P, QUARTERS, D], U32, align_bytes=64)
-            nc.sync.dma_start(out=w2[:].bitcast(I32), in_=w2_dram[a].bitcast(I32))
+            step = QUARTERS // pieces
+            for j in range(0, QUARTERS, step):
+                nc.sync.dma_start(
+                    out=w2[:, j : j + step, :].bitcast(I32), in_=w2_dram[a][:, j : j + step, :].bitcast(I32)
+                )
             w2_tiles[a] = w2
 
-        load_w1(0, QUARTERS)
-        for a in range(1, W1_AHEAD):
-            load_w1(a, 1)
+        load_w1(0, 0, 1)
+        load_w1_scales(0, HEAD_CHUNKS)
+        load_w1(0, 1, QUARTERS)
+        nc.sync.dma_start(out=tail_rows[0:1, :], in_=b2g.rearrange("(o n) -> o n", o=1))
+        nc.sync.dma_start(out=tail_rows[1:2, :], in_=bv.rearrange("(o n) -> o n", o=1))
+        load_w1(1)
+        load_w1(2)
+        load_w1_scales(HEAD_CHUNKS, CHUNKS)
         wv_words = consts.tile([P, D], U32, align_bytes=64)
         for a in range(CHUNKS):
-            load_w2(a)
-            if a + W1_AHEAD < CHUNKS:
-                load_w1(a + W1_AHEAD, 1)
-            if a + W1_AHEAD == CHUNKS:
+            load_w2_scales(a)
+            load_w2(a, QUARTERS if a == CHUNKS - 1 else 1)
+            if a == WV_BEHIND:
                 for quadrant in range(4):
                     nc.sync.dma_start(
                         out=wv_plane[32 * quadrant : 32 * quadrant + 4, :].bitcast(I32),
                         in_=Wv_scales[0][4 * quadrant : 4 * quadrant + 4, :].bitcast(I32),
                     )
+            if a + W1_AHEAD < CHUNKS:
+                load_w1(a + W1_AHEAD)
+            if a == WV_BEHIND:
                 nc.sync.dma_start(
                     out=wv_words[:].bitcast(I32), in_=Wv_words[0].rearrange("p n t -> p (n t)").bitcast(I32)
                 )
@@ -140,26 +149,42 @@ def tile_selectivemixing_pa_k_kernel(
         bias_flipped = psum_z.tile([P, 2, P], F32, tag="z")
         for u in range(2):
             nc.tensor.transpose(bias_flipped[:, u, :], bias_words[:, u, :], ident_f32[:])
-        bias_cols = consts.tile([P, 2, P], F32)
-        nc.scalar.copy(out=bias_cols[:], in_=bias_flipped[:])
+        bias_cols = consts.tile([P, 2, GROUPS], F32)
+        nc.scalar.copy(out=bias_cols[:], in_=bias_flipped[:, :, 0:GROUPS])
 
         x_codes = consts.tile([P, TOKENS], U32, align_bytes=64)
         x_plane = consts.tile([P, TOKENS], U8, align_bytes=64)
         b1_cols = consts.tile([P, GROUPS, PACK], F32)
 
         tail_bias = consts.tile([P, 2, D], BF16)
-        spread = psum_z.tile([P, 2, 2, P], F32, tag="z")
-        for i in range(2):
+
+        tail_cols = consts.tile([P, 2, 2], F32)
+        tail_words = tail_rows[:].bitcast(F32).rearrange("c (q u) -> c u q", u=2)
+        tail_psum = {}
+
+        def flip_tail_biases():
+            flipped = psum_z.tile([P, 2, P], F32, tag="z")
             for u in range(2):
-                nc.tensor.transpose(
-                    spread[:, i, u, :],
-                    bias_cols[:, u, GROUPS + i : GROUPS + i + 1].to_broadcast([P, P]),
-                    ident_f32[:],
-                )
-        nc.scalar.copy(
-            out=tail_bias[:].bitcast(F32).rearrange("p i (q u) -> p i q u", u=2),
-            in_=spread[:].rearrange("p i u q -> p i q u"),
-        )
+                nc.tensor.transpose(flipped[:, u, :], tail_words[:, u, :], ident_f32[:])
+            tail_psum["flipped"] = flipped
+
+        def copy_tail_columns():
+            nc.scalar.copy(out=tail_cols[:], in_=tail_psum["flipped"][:, :, 0:2])
+
+        def spread_tail_biases():
+            spread = psum_z.tile([P, 2, 2, P], F32, tag="z")
+            for i in range(2):
+                for u in range(2):
+                    nc.tensor.transpose(
+                        spread[:, i, u, :], tail_cols[:, u, i : i + 1].to_broadcast([P, P]), ident_f32[:]
+                    )
+            tail_psum["spread"] = spread
+
+        def copy_tail_biases():
+            nc.scalar.copy(
+                out=tail_bias[:].bitcast(F32).rearrange("p i (q u) -> p i q u", u=2),
+                in_=tail_psum["spread"][:].rearrange("p i u q -> p i q u"),
+            )
 
         w1_sorted = {}
         z_tiles = {}
@@ -288,7 +313,7 @@ def tile_selectivemixing_pa_k_kernel(
                 if s + 3 == 0:
                     nc.vector.tensor_copy(
                         out=b1_cols[:].rearrange("p c (u e) -> p c u e", u=2),
-                        in_=bias_cols[:].bitcast(BF16).rearrange("p u (c e) -> p c u e", e=2)[:, 0:GROUPS],
+                        in_=bias_cols[:].bitcast(BF16).rearrange("p u (c e) -> p c u e", e=2),
                     )
             elif s >= GROUPS - 2:
                 value_bias(s - (GROUPS - 2))
@@ -307,6 +332,12 @@ def tile_selectivemixing_pa_k_kernel(
                 seconds += 1
             if s >= 0:
                 silu(s)
+            if s == 0:
+                flip_tail_biases()
+                copy_tail_columns()
+            if s == 1:
+                spread_tail_biases()
+                copy_tail_biases()
             if on_scalar(s - 1):
                 new_tiles(s - 1)
                 interleave(s - 1)

@@ -26,7 +26,7 @@ W1_AHEAD = 3
 HEAD_CHUNKS = 2
 WV_BEHIND = 3
 SECOND_START = 7
-SCALAR_EVERY = 11
+SCALAR_EVERY = 64
 
 FLOPS = 2 * TOKENS * (D * F + F * D + D * D)
 
@@ -66,9 +66,11 @@ def tile_selectivemixing_pa_k_kernel(
 
         ident_f32 = consts.tile([P, P], F32)
         make_identity(nc, ident_f32[:])
+        nc.gpsimd.dma_start(out=tail_rows[0:1, :], in_=b2g.rearrange("(o n) -> o n", o=1))
+        nc.gpsimd.dma_start(out=tail_rows[1:2, :], in_=bv.rearrange("(o n) -> o n", o=1))
 
         x_sb = consts.tile([P, TOKEN_TILES, D], BF16)
-        nc.scalar.dma_start(out=x_sb[:], in_=x_rows.rearrange("(t p) d -> p t d", p=P))
+        nc.sync.dma_start(out=x_sb[:], in_=x_rows.rearrange("(t p) d -> p t d", p=P))
         nc.scalar.dma_start(out=bias_rows[0:GROUPS, :], in_=b1.rearrange("(g n) -> g n", n=D))
         nc.scalar.activation(out=warm[:], in_=zero[:], func=ACT.Silu)
 
@@ -109,11 +111,9 @@ def tile_selectivemixing_pa_k_kernel(
                 )
             w2_tiles[a] = w2
 
-        load_w1(0, 0, 1)
         load_w1_scales(0, HEAD_CHUNKS)
+        load_w1(0, 0, 1)
         load_w1(0, 1, QUARTERS)
-        nc.sync.dma_start(out=tail_rows[0:1, :], in_=b2g.rearrange("(o n) -> o n", o=1))
-        nc.sync.dma_start(out=tail_rows[1:2, :], in_=bv.rearrange("(o n) -> o n", o=1))
         load_w1(1)
         load_w1(2)
         load_w1_scales(HEAD_CHUNKS, CHUNKS)
@@ -160,30 +160,27 @@ def tile_selectivemixing_pa_k_kernel(
 
         tail_cols = consts.tile([P, 2, 2], F32)
         tail_words = tail_rows[:].bitcast(F32).rearrange("c (q u) -> c u q", u=2)
-        tail_psum = {}
 
         def flip_tail_biases():
-            flipped = psum_z.tile([P, 2, P], F32, tag="z")
             for u in range(2):
-                nc.tensor.transpose(flipped[:, u, :], tail_words[:, u, :], ident_f32[:])
-            tail_psum["flipped"] = flipped
+                nc.tensor.transpose(acc[0][:, P * u : P * (u + 1)], tail_words[:, u, :], ident_f32[:])
 
         def copy_tail_columns():
-            nc.scalar.copy(out=tail_cols[:], in_=tail_psum["flipped"][:, :, 0:2])
+            nc.scalar.copy(out=tail_cols[:], in_=acc[0][:, 0 : 2 * P].rearrange("p (u c) -> p u c", u=2)[:, :, 0:2])
 
         def spread_tail_biases():
-            spread = psum_z.tile([P, 2, 2, P], F32, tag="z")
             for i in range(2):
                 for u in range(2):
                     nc.tensor.transpose(
-                        spread[:, i, u, :], tail_cols[:, u, i : i + 1].to_broadcast([P, P]), ident_f32[:]
+                        acc[1][:, P * (2 * i + u) : P * (2 * i + u + 1)],
+                        tail_cols[:, u, i : i + 1].to_broadcast([P, P]),
+                        ident_f32[:],
                     )
-            tail_psum["spread"] = spread
 
         def copy_tail_biases():
             nc.scalar.copy(
                 out=tail_bias[:].bitcast(F32).rearrange("p i (q u) -> p i q u", u=2),
-                in_=tail_psum["spread"][:].rearrange("p i u q -> p i q u"),
+                in_=acc[1][:].rearrange("p (i u q) -> p i q u", i=2, u=2),
             )
 
         w1_sorted = {}
@@ -332,11 +329,13 @@ def tile_selectivemixing_pa_k_kernel(
                 seconds += 1
             if s >= 0:
                 silu(s)
-            if s == 0:
-                flip_tail_biases()
-                copy_tail_columns()
             if s == 1:
+                flip_tail_biases()
+            if s == 2:
+                copy_tail_columns()
+            if s == 3:
                 spread_tail_biases()
+            if s == 4:
                 copy_tail_biases()
             if on_scalar(s - 1):
                 new_tiles(s - 1)

@@ -26,7 +26,6 @@ W1_AHEAD = 3
 HEAD_CHUNKS = 2
 WV_BEHIND = 3
 SECOND_START = 7
-SCALAR_EVERY = 64
 
 FLOPS = 2 * TOKENS * (D * F + F * D + D * D)
 
@@ -194,14 +193,15 @@ def tile_selectivemixing_pa_k_kernel(
         def sort_planes(a):
             nc.vector.tensor_copy(out=w1_planes[:, a, :, :], in_=w1_planes_raw[:, a, :, :].rearrange("p m t -> p t m"))
 
-        def sort_codes(i):
+        def sort_codes(i, count):
             a, j = i // QUARTERS, i % QUARTERS
-            w1s = work.tile([P, D], U32, align_bytes=64, bufs=4)
+            w1s = work.tile([P, PACK, count * P], U32, align_bytes=64, bufs=4)
             nc.vector.tensor_copy(
-                out=w1s[:].bitcast(I32).rearrange("p (t m) -> p m t", t=PACK),
-                in_=w1_tiles[a][:, j, :].bitcast(I32).rearrange("p (m t) -> p m t", t=PACK),
+                out=w1s[:].bitcast(I32).rearrange("p t m -> p m t"),
+                in_=w1_tiles[a][:, j : j + count, :].rearrange("p j n -> p (j n)").bitcast(I32).rearrange("p (m t) -> p m t", t=PACK),
             )
-            w1_sorted[i] = w1s
+            for k in range(count):
+                w1_sorted[i + k] = w1s[:, :, P * k : P * (k + 1)]
 
         def first_layer(i):
             a, j = i // QUARTERS, i % QUARTERS
@@ -211,7 +211,7 @@ def tile_selectivemixing_pa_k_kernel(
                     t = 2 * half + s
                     nc.tensor.matmul_mx(
                         out=z[:, s, :],
-                        lhsT=w1_sorted[i][:, P * t : P * (t + 1)].bitcast(FP8X4),
+                        lhsT=w1_sorted[i][:, t, :].bitcast(FP8X4),
                         lhsT_scale=w1_planes[4 * j : P, a, t, :],
                         rhs=x_codes[:].bitcast(FP8X4),
                         rhs_scale=x_plane[:],
@@ -220,53 +220,54 @@ def tile_selectivemixing_pa_k_kernel(
                     )
                 z_tiles[(i, half)] = z
 
+        def span(i):
+            return (i - i % 2, 2) if i < GROUPS - 2 else (i, 1)
+
         def silu(i):
             g = CHUNKS * (i % QUARTERS) + i // QUARTERS
-            h = work.tile([P, PACK, TOKENS], BF16)
+            first, count = span(i)
+            if i == first:
+                h_tiles[first] = work.tile([P, PACK, count * TOKENS], BF16, name="h")
             pieces = TOKEN_TILES if i == GROUPS - 1 else 1
             width = TOKENS // pieces
+            base = TOKENS * (i - first)
             for n0 in range(0, TOKENS, width):
                 for t in range(PACK):
                     nc.scalar.activation(
-                        out=h[:, t, n0 : n0 + width],
+                        out=h_tiles[first][:, t, base + n0 : base + n0 + width],
                         in_=z_tiles[(i, t // 2)][:, t % 2, n0 : n0 + width],
                         func=ACT.Silu,
                         bias=b1_cols[:, g, t : t + 1],
                     )
-            h_tiles[i] = h
 
-        def new_tiles(i):
-            grouped = work.tile([P, TOKENS * PACK], BF16, align_bytes=64)
-            codes = work.tile([P, TOKENS], U32, align_bytes=64, bufs=12)
-            plane = work.tile([P, TOKENS], U8, align_bytes=64, bufs=12)
-            grouped_tiles[i] = grouped
-            h_codes[i] = codes
-            h_planes[i] = plane
+        def new_tiles(first):
+            width = TOKENS * span(first)[1]
+            grouped_tiles[first] = work.tile([P, width * PACK], BF16, align_bytes=64, name="grouped")
+            h_codes[first] = work.tile([P, width], U32, align_bytes=64, bufs=7, name="codes")
+            h_planes[first] = work.tile([P, width], U8, align_bytes=64, bufs=7, name="plane")
 
-        def on_scalar(i):
-            return i >= 0 and i % SCALAR_EVERY == SCALAR_EVERY - 1
-
-        def interleave(i, n0=0, width=TOKENS):
-            copy = nc.scalar.copy if on_scalar(i) else nc.vector.tensor_copy
-            copy(
-                out=grouped_tiles[i][:, PACK * n0 : PACK * (n0 + width)].rearrange("p (c i t) -> p c t i", i=4, t=PACK),
-                in_=h_tiles[i][:, :, n0 : n0 + width].rearrange("p t (c i) -> p c t i", i=4),
+        def interleave(first, n0, width):
+            nc.vector.tensor_copy(
+                out=grouped_tiles[first][:, PACK * n0 : PACK * (n0 + width)].rearrange("p (c i t) -> p c t i", i=4, t=PACK),
+                in_=h_tiles[first][:, :, n0 : n0 + width].rearrange("p t (c i) -> p c t i", i=4),
             )
 
-        def quantise(i, n0=0, width=TOKENS):
+        def quantise(first, n0, width):
             nc.vector.quantize_mx(
-                out=h_codes[i][:, n0 : n0 + width].bitcast(FP8X4),
-                scales=h_planes[i][:, n0 : n0 + width],
-                in_=grouped_tiles[i][:, PACK * n0 : PACK * (n0 + width)],
+                out=h_codes[first][:, n0 : n0 + width].bitcast(FP8X4),
+                scales=h_planes[first][:, n0 : n0 + width],
+                in_=grouped_tiles[first][:, PACK * n0 : PACK * (n0 + width)],
             )
 
         def second_layer(i, tiles=(0, 1)):
             a, j = i // QUARTERS, i % QUARTERS
+            first = span(i)[0]
+            base = TOKENS * (i - first)
             for t in tiles:
                 nc.tensor.matmul_mx(
                     out=acc[t][:],
-                    lhsT=h_codes[i][:, P * t : P * (t + 1)].bitcast(FP8X4),
-                    lhsT_scale=h_planes[i][:, P * t : P * (t + 1)],
+                    lhsT=h_codes[first][:, base + P * t : base + P * (t + 1)].bitcast(FP8X4),
+                    lhsT_scale=h_planes[first][:, base + P * t : base + P * (t + 1)],
                     rhs=w2_tiles[a][:, j, :].bitcast(FP8X4),
                     rhs_scale=w2_planes[4 * j : P, a, :],
                     start=(i == 0),
@@ -294,29 +295,31 @@ def tile_selectivemixing_pa_k_kernel(
 
         seconds = 0
         quantised = 0
+        sorts = {-3: (0, 1), -2: (1, 1), -1: (2, 2)}
+        for i in range(4, GROUPS, 2):
+            sorts[i - 4] = (i, 2)
         for s in range(-3, GROUPS):
-            if on_scalar(s - 2):
-                quantise(s - 2)
-                quantised = s - 1
-            if s >= 1 and not on_scalar(s - 1):
-                new_tiles(s - 1)
-                interleave(s - 1)
-            if s + 3 < GROUPS:
-                if (s + 3) % QUARTERS == 0:
-                    sort_planes((s + 3) // QUARTERS)
-                if s + 3 == 0:
+            ready = span(s - 1) if s >= 2 and (s % 2 == 0 or s == GROUPS - 1) else None
+            if ready:
+                new_tiles(ready[0])
+                interleave(ready[0], 0, ready[1] * TOKENS)
+            if s in sorts:
+                i, count = sorts[s]
+                if i % QUARTERS == 0:
+                    sort_planes(i // QUARTERS)
+                if i == 0:
                     nc.vector.quantize_mx(out=x_codes[:].bitcast(FP8X4), scales=x_plane[:], in_=x_grouped[:])
-                sort_codes(s + 3)
-                if s + 3 == 0:
+                sort_codes(i, count)
+                if i == 0:
                     nc.vector.tensor_copy(
                         out=b1_cols[:].rearrange("p c (u e) -> p c u e", u=2),
                         in_=bias_cols[:].bitcast(BF16).rearrange("p u (c e) -> p c u e", e=2),
                     )
             elif s >= GROUPS - 2:
                 value_bias(s - (GROUPS - 2))
-            if s >= 1 and not on_scalar(s - 1):
-                quantise(s - 1)
-                quantised = s
+            if ready:
+                quantise(ready[0], 0, ready[1] * TOKENS)
+                quantised = ready[0] + ready[1]
             if 0 <= s + 2 < GROUPS - 1:
                 first_layer(s + 2)
             elif s + 2 == GROUPS - 1:
@@ -337,9 +340,6 @@ def tile_selectivemixing_pa_k_kernel(
                 spread_tail_biases()
             if s == 4:
                 copy_tail_biases()
-            if on_scalar(s - 1):
-                new_tiles(s - 1)
-                interleave(s - 1)
         nc.scalar.activation(out=warm[:], in_=zero[:], func=ACT.Sigmoid)
         while seconds < GROUPS - 1:
             second_layer(seconds)

@@ -24,7 +24,6 @@ QUARTERS = 4
 CHUNKS = GROUPS // QUARTERS
 W1_AHEAD = 3
 HEAD_CHUNKS = 2
-WV_BEHIND = 3
 SECOND_START = 7
 
 FLOPS = 2 * TOKENS * (D * F + F * D + D * D)
@@ -65,8 +64,6 @@ def tile_selectivemixing_pa_k_kernel(
 
         ident_f32 = consts.tile([P, P], F32)
         make_identity(nc, ident_f32[:])
-        nc.gpsimd.dma_start(out=tail_rows[0:1, :], in_=b2g.rearrange("(o n) -> o n", o=1))
-        nc.gpsimd.dma_start(out=tail_rows[1:2, :], in_=bv.rearrange("(o n) -> o n", o=1))
 
         x_sb = consts.tile([P, TOKEN_TILES, D], BF16)
         nc.sync.dma_start(out=x_sb[:], in_=x_rows.rearrange("(t p) d -> p t d", p=P))
@@ -110,39 +107,40 @@ def tile_selectivemixing_pa_k_kernel(
                 )
             w2_tiles[a] = w2
 
-        load_w1_scales(0, HEAD_CHUNKS)
         load_w1(0, 0, 1)
+        load_w1_scales(0, HEAD_CHUNKS)
         load_w1(0, 1, QUARTERS)
         load_w1(1)
-        load_w1(2)
+        nc.sync.dma_start(out=tail_rows[0:1, :], in_=b2g.rearrange("(o n) -> o n", o=1))
+        nc.sync.dma_start(out=tail_rows[1:2, :], in_=bv.rearrange("(o n) -> o n", o=1))
         load_w1_scales(HEAD_CHUNKS, CHUNKS)
+        load_w1(2)
         wv_words = consts.tile([P, D], U32, align_bytes=64)
         for a in range(CHUNKS):
             load_w2_scales(a)
             load_w2(a, QUARTERS if a == CHUNKS - 1 else 1)
-            if a == WV_BEHIND:
-                for quadrant in range(4):
-                    nc.sync.dma_start(
-                        out=wv_plane[32 * quadrant : 32 * quadrant + 4, :].bitcast(I32),
-                        in_=Wv_scales[0][4 * quadrant : 4 * quadrant + 4, :].bitcast(I32),
-                    )
+            if a < 4:
+                nc.sync.dma_start(
+                    out=wv_plane[32 * a : 32 * a + 4, :].bitcast(I32),
+                    in_=Wv_scales[0][4 * a : 4 * a + 4, :].bitcast(I32),
+                )
             if a + W1_AHEAD < CHUNKS:
                 load_w1(a + W1_AHEAD)
-            if a == WV_BEHIND:
+            if a == 4:
                 nc.sync.dma_start(
                     out=wv_words[:].bitcast(I32), in_=Wv_words[0].rearrange("p n t -> p (n t)").bitcast(I32)
                 )
 
         x_words = x_sb[:].bitcast(F32).rearrange("p t (q u) -> p t u q", u=2)
-        x_flipped = psum_z.tile([P, TOKEN_TILES, 2, P], F32, tag="z")
-        for t in range(TOKEN_TILES):
-            for u in range(2):
-                nc.tensor.transpose(x_flipped[:, t, u, :], x_words[:, t, u, :], ident_f32[:])
         x_grouped = consts.tile([P, TOKENS * PACK], BF16, align_bytes=64)
-        nc.vector.tensor_copy(
-            out=x_grouped[:].bitcast(F32).rearrange("p (t k u) -> p t k u", t=TOKEN_TILES, u=2),
-            in_=x_flipped[:].rearrange("p t u k -> p t k u"),
-        )
+        for t in range(TOKEN_TILES):
+            x_flipped = psum_z.tile([P, 2, P], F32, tag="z")
+            for u in range(2):
+                nc.tensor.transpose(x_flipped[:, u, :], x_words[:, t, u, :], ident_f32[:])
+            nc.scalar.copy(
+                out=x_grouped[:, PACK * P * t : PACK * P * (t + 1)].bitcast(F32).rearrange("p (k u) -> p k u", u=2),
+                in_=x_flipped[:].rearrange("p u k -> p k u"),
+            )
 
         bias_words = bias_rows[:].bitcast(F32).rearrange("c (q u) -> c u q", u=2)
         bias_flipped = psum_z.tile([P, 2, P], F32, tag="z")
@@ -165,7 +163,7 @@ def tile_selectivemixing_pa_k_kernel(
                 nc.tensor.transpose(acc[0][:, P * u : P * (u + 1)], tail_words[:, u, :], ident_f32[:])
 
         def copy_tail_columns():
-            nc.scalar.copy(out=tail_cols[:], in_=acc[0][:, 0 : 2 * P].rearrange("p (u c) -> p u c", u=2)[:, :, 0:2])
+            nc.vector.tensor_copy(out=tail_cols[:], in_=acc[0][:, 0 : 2 * P].rearrange("p (u c) -> p u c", u=2)[:, :, 0:2])
 
         def spread_tail_biases():
             for i in range(2):
@@ -177,7 +175,7 @@ def tile_selectivemixing_pa_k_kernel(
                     )
 
         def copy_tail_biases():
-            nc.scalar.copy(
+            nc.vector.tensor_copy(
                 out=tail_bias[:].bitcast(F32).rearrange("p i (q u) -> p i q u", u=2),
                 in_=acc[1][:].rearrange("p (i u q) -> p i q u", i=2, u=2),
             )
@@ -305,12 +303,11 @@ def tile_selectivemixing_pa_k_kernel(
                 interleave(ready[0], 0, ready[1] * TOKENS)
             if s in sorts:
                 i, count = sorts[s]
+                sort_codes(i, count)
                 if i % QUARTERS == 0:
                     sort_planes(i // QUARTERS)
                 if i == 0:
                     nc.vector.quantize_mx(out=x_codes[:].bitcast(FP8X4), scales=x_plane[:], in_=x_grouped[:])
-                sort_codes(i, count)
-                if i == 0:
                     nc.vector.tensor_copy(
                         out=b1_cols[:].rearrange("p c (u e) -> p c u e", u=2),
                         in_=bias_cols[:].bitcast(BF16).rearrange("p u (c e) -> p c u e", e=2),
@@ -332,13 +329,12 @@ def tile_selectivemixing_pa_k_kernel(
                 seconds += 1
             if s >= 0:
                 silu(s)
-            if s == 1:
-                flip_tail_biases()
-            if s == 2:
-                copy_tail_columns()
             if s == 3:
-                spread_tail_biases()
+                flip_tail_biases()
+                copy_tail_columns()
             if s == 4:
+                spread_tail_biases()
+            if s == 5:
                 copy_tail_biases()
         nc.scalar.activation(out=warm[:], in_=zero[:], func=ACT.Sigmoid)
         while seconds < GROUPS - 1:

@@ -24,7 +24,8 @@ QUARTERS = 4
 CHUNKS = GROUPS // QUARTERS
 W1_AHEAD = 3
 HEAD_CHUNKS = 2
-SECOND_START = 7
+WV_BEHIND = 3
+SECOND_START = 8
 
 FLOPS = 2 * TOKENS * (D * F + F * D + D * D)
 
@@ -64,6 +65,8 @@ def tile_selectivemixing_pa_k_kernel(
 
         ident_f32 = consts.tile([P, P], F32)
         make_identity(nc, ident_f32[:])
+        nc.gpsimd.dma_start(out=tail_rows[0:1, :], in_=b2g.rearrange("(o n) -> o n", o=1))
+        nc.gpsimd.dma_start(out=tail_rows[1:2, :], in_=bv.rearrange("(o n) -> o n", o=1))
 
         x_sb = consts.tile([P, TOKEN_TILES, D], BF16)
         nc.sync.dma_start(out=x_sb[:], in_=x_rows.rearrange("(t p) d -> p t d", p=P))
@@ -111,22 +114,21 @@ def tile_selectivemixing_pa_k_kernel(
         load_w1_scales(0, HEAD_CHUNKS)
         load_w1(0, 1, QUARTERS)
         load_w1(1)
-        nc.sync.dma_start(out=tail_rows[0:1, :], in_=b2g.rearrange("(o n) -> o n", o=1))
-        nc.sync.dma_start(out=tail_rows[1:2, :], in_=bv.rearrange("(o n) -> o n", o=1))
-        load_w1_scales(HEAD_CHUNKS, CHUNKS)
         load_w1(2)
+        load_w1_scales(HEAD_CHUNKS, CHUNKS)
         wv_words = consts.tile([P, D], U32, align_bytes=64)
         for a in range(CHUNKS):
             load_w2_scales(a)
             load_w2(a, QUARTERS if a == CHUNKS - 1 else 1)
-            if a < 4:
-                nc.sync.dma_start(
-                    out=wv_plane[32 * a : 32 * a + 4, :].bitcast(I32),
-                    in_=Wv_scales[0][4 * a : 4 * a + 4, :].bitcast(I32),
-                )
+            if a == WV_BEHIND:
+                for quadrant in range(4):
+                    nc.sync.dma_start(
+                        out=wv_plane[32 * quadrant : 32 * quadrant + 4, :].bitcast(I32),
+                        in_=Wv_scales[0][4 * quadrant : 4 * quadrant + 4, :].bitcast(I32),
+                    )
             if a + W1_AHEAD < CHUNKS:
                 load_w1(a + W1_AHEAD)
-            if a == 4:
+            if a == WV_BEHIND:
                 nc.sync.dma_start(
                     out=wv_words[:].bitcast(I32), in_=Wv_words[0].rearrange("p n t -> p (n t)").bitcast(I32)
                 )
@@ -329,12 +331,12 @@ def tile_selectivemixing_pa_k_kernel(
                 seconds += 1
             if s >= 0:
                 silu(s)
-            if s == 3:
+            if s == 5:
                 flip_tail_biases()
                 copy_tail_columns()
-            if s == 4:
+            if s == 6:
                 spread_tail_biases()
-            if s == 5:
+            if s == 7:
                 copy_tail_biases()
         nc.scalar.activation(out=warm[:], in_=zero[:], func=ACT.Sigmoid)
         while seconds < GROUPS - 1:

@@ -25,7 +25,7 @@ CHUNKS = GROUPS // QUARTERS
 W1_AHEAD = 3
 HEAD_CHUNKS = 2
 WV_BEHIND = 3
-SECOND_START = 8
+SECOND_START = 7
 
 FLOPS = 2 * TOKENS * (D * F + F * D + D * D)
 
@@ -326,7 +326,7 @@ def tile_selectivemixing_pa_k_kernel(
                     value_product(t)
             elif s + 2 == GROUPS:
                 first_layer(GROUPS - 1)
-            while seconds < quantised and 4 * seconds <= 5 * (s - SECOND_START):
+            while seconds < quantised and seconds <= s - SECOND_START:
                 second_layer(seconds)
                 seconds += 1
             if s >= 0:
@@ -336,7 +336,6 @@ def tile_selectivemixing_pa_k_kernel(
                 copy_tail_columns()
             if s == 6:
                 spread_tail_biases()
-            if s == 7:
                 copy_tail_biases()
         nc.scalar.activation(out=warm[:], in_=zero[:], func=ACT.Sigmoid)
         while seconds < GROUPS - 1:

@@ -101,9 +101,12 @@ def tile_selectivemixing_pa_k_kernel(
                     in_=w2_scale_chunks[a][:, 4 * quadrant : 4 * quadrant + 4, :],
                 )
 
-        def load_w2(a, pieces=1):
+        def load_w1_halves(a):
+            load_w1(a, 0, 2)
+            load_w1(a, 2, QUARTERS)
+
+        def load_w2(a, step):
             w2 = weights.tile([P, QUARTERS, D], U32, align_bytes=64)
-            step = QUARTERS // pieces
             for j in range(0, QUARTERS, step):
                 nc.sync.dma_start(
                     out=w2[:, j : j + step, :].bitcast(I32), in_=w2_dram[a][:, j : j + step, :].bitcast(I32)
@@ -113,13 +116,13 @@ def tile_selectivemixing_pa_k_kernel(
         load_w1(0, 0, 1)
         load_w1_scales(0, HEAD_CHUNKS)
         load_w1(0, 1, QUARTERS)
-        load_w1(1)
-        load_w1(2)
+        for a in range(1, W1_AHEAD):
+            load_w1_halves(a)
         load_w1_scales(HEAD_CHUNKS, CHUNKS)
         wv_words = consts.tile([P, D], U32, align_bytes=64)
         for a in range(CHUNKS):
             load_w2_scales(a)
-            load_w2(a, QUARTERS if a == CHUNKS - 1 else 1)
+            load_w2(a, 1 if a == CHUNKS - 1 else 2)
             if a == WV_BEHIND:
                 for quadrant in range(4):
                     nc.sync.dma_start(
@@ -127,7 +130,7 @@ def tile_selectivemixing_pa_k_kernel(
                         in_=Wv_scales[0][4 * quadrant : 4 * quadrant + 4, :].bitcast(I32),
                     )
             if a + W1_AHEAD < CHUNKS:
-                load_w1(a + W1_AHEAD)
+                load_w1_halves(a + W1_AHEAD)
             if a == WV_BEHIND:
                 nc.sync.dma_start(
                     out=wv_words[:].bitcast(I32), in_=Wv_words[0].rearrange("p n t -> p (n t)").bitcast(I32)

@@ -224,7 +224,7 @@ def tile_selectivemixing_pa_k_kernel(
                 z_tiles[(i, half)] = z
 
         def span(i):
-            return (i - i % 2, 2) if i < GROUPS - 2 else (i, 1)
+            return (i - i % 2, 2) if 4 <= i < GROUPS - 2 else (i, 1)
 
         def silu(i):
             g = CHUNKS * (i % QUARTERS) + i // QUARTERS
@@ -302,7 +302,7 @@ def tile_selectivemixing_pa_k_kernel(
         for i in range(4, GROUPS, 2):
             sorts[i - 4] = (i, 2)
         for s in range(-3, GROUPS):
-            ready = span(s - 1) if s >= 2 and (s % 2 == 0 or s == GROUPS - 1) else None
+            ready = span(s - 1) if s >= 1 and sum(span(s - 1)) == s else None
             if ready:
                 new_tiles(ready[0])
                 interleave(ready[0], 0, ready[1] * TOKENS)
@@ -341,14 +341,21 @@ def tile_selectivemixing_pa_k_kernel(
                 spread_tail_biases()
                 copy_tail_biases()
         nc.scalar.activation(out=warm[:], in_=zero[:], func=ACT.Sigmoid)
-        while seconds < GROUPS - 1:
-            second_layer(seconds)
-            seconds += 1
-        new_tiles(GROUPS - 1)
-        for t in range(TOKEN_TILES):
-            interleave(GROUPS - 1, P * t, P)
-            quantise(GROUPS - 1, P * t, P)
-            second_layer(GROUPS - 1, (t,))
+        for i in range(seconds, GROUPS - QUARTERS):
+            second_layer(i)
+        last = GROUPS - 1
+        for i in range(GROUPS - QUARTERS, last):
+            second_layer(i, (0,))
+        second_layer(last - 3, (1,))
+        new_tiles(last)
+        interleave(last, 0, P)
+        quantise(last, 0, P)
+        second_layer(last, (0,))
+        second_layer(last - 2, (1,))
+        second_layer(last - 1, (1,))
+        interleave(last, P, P)
+        quantise(last, P, P)
+        second_layer(last, (1,))
 
         gates = {}
         half = D // 2

from contextlib import ExitStack

import concourse.mybir as mybir
from concourse.masks import make_identity

F32 = mybir.dt.float32
BF16 = mybir.dt.bfloat16
I32 = mybir.dt.int32
U32 = mybir.dt.uint32
U8 = mybir.dt.uint8
FP8X4 = mybir.dt.float8_e4m3fn_x4
ACT = mybir.ActivationFunctionType
ADD = mybir.AluOpType.add
MULT = mybir.AluOpType.mult

P = 128
PACK = 4
TOKENS = 256
TOKEN_TILES = TOKENS // P
D = 512
F = 16384
GROUPS = F // D
QUARTERS = 4
CHUNKS = GROUPS // QUARTERS
W1_AHEAD = 3
HEAD_CHUNKS = 2
WV_BEHIND = 3
SECOND_START = 7

FLOPS = 2 * TOKENS * (D * F + F * D + D * D)


def tile_selectivemixing_pa_k_kernel(
    tc, x, W1_words, W1_scales, b1, W2g_words, W2g_scales, b2g, Wv_words, Wv_scales, bv, out
):
    nc = tc.nc
    x_rows = x.flatten_outer_dims()
    out_rows = out.flatten_outer_dims()
    w1_dram = W1_words[0].rearrange("p n t -> p (n t)").bitcast(I32).rearrange("p (j a n) -> p j a n", j=QUARTERS, a=CHUNKS)
    w2_dram = W2g_words.rearrange("(j a) p n t -> a p j (n t)", j=QUARTERS)

    with ExitStack() as stack:
        consts = stack.enter_context(tc.tile_pool(name="consts", bufs=1))
        weights = stack.enter_context(tc.tile_pool(name="weights", bufs=CHUNKS))
        work = stack.enter_context(tc.tile_pool(name="work", bufs=3))
        psum_acc = stack.enter_context(tc.psum_pool(name="psum_acc", bufs=1))
        psum_z = stack.enter_context(tc.psum_pool(name="psum_z", bufs=6))
        stack.enter_context(tc.manual_schedule())

        w1_planes_raw = consts.tile([P, CHUNKS, P, PACK], U8, align_bytes=64)
        w1_planes = consts.tile([P, CHUNKS, PACK, P], U8, align_bytes=64)
        bias_rows = consts.tile([P, D], BF16)
        tail_rows = consts.tile([P, D], BF16)
        w2_planes = consts.tile([P, CHUNKS, D], U8, align_bytes=64)
        wv_plane = consts.tile([P, D], U8, align_bytes=64)
        zero = consts.tile([P, 1], F32)
        warm = consts.tile([P, 1], F32)
        nc.vector.memset(w1_planes_raw[:, 0:HEAD_CHUNKS].rearrange("p a m t -> p (a m t)").bitcast(I32), 0)
        nc.vector.memset(zero[:], 0.0)
        nc.vector.memset(bias_rows[:].bitcast(I32), 0)
        nc.vector.memset(tail_rows[:].bitcast(I32), 0)
        nc.vector.memset(w1_planes_raw[:, HEAD_CHUNKS:CHUNKS].rearrange("p a m t -> p (a m t)").bitcast(I32), 0)
        nc.vector.memset(w2_planes[:].bitcast(I32), 0)
        nc.vector.memset(wv_plane[:].bitcast(I32), 0)

        ident_f32 = consts.tile([P, P], F32)
        make_identity(nc, ident_f32[:])
        nc.gpsimd.dma_start(out=tail_rows[0:1, :], in_=b2g.rearrange("(o n) -> o n", o=1))
        nc.gpsimd.dma_start(out=tail_rows[1:2, :], in_=bv.rearrange("(o n) -> o n", o=1))

        x_sb = consts.tile([P, TOKEN_TILES, D], BF16)
        nc.sync.dma_start(out=x_sb[:], in_=x_rows.rearrange("(t p) d -> p t d", p=P))
        nc.scalar.dma_start(out=bias_rows[0:GROUPS, :], in_=b1.rearrange("(g n) -> g n", n=D))
        nc.scalar.activation(out=warm[:], in_=zero[:], func=ACT.Silu)

        w1_scale_quarters = W1_scales[0].bitcast(I32).rearrange("q (j n) -> j q n", j=QUARTERS)

        w1_tiles = {}
        w2_tiles = {}

        def load_w1(a, j0=0, j1=QUARTERS):
            if j0 == 0:
                w1_tiles[a] = weights.tile([P, QUARTERS, D], U32, align_bytes=64, name="w1")
            nc.sync.dma_start(out=w1_tiles[a][:, j0:j1, :].bitcast(I32), in_=w1_dram[:, j0:j1, a, :])

        def load_w1_scales(a0, a1):
            for quadrant in range(4):
                nc.sync.dma_start(
                    out=w1_planes_raw[32 * quadrant : 32 * quadrant + 16, a0:a1]
                    .rearrange("p a m t -> p (a m t)")
                    .bitcast(I32),
                    in_=w1_scale_quarters[:, 4 * quadrant : 4 * quadrant + 4, P * a0 : P * a1],
                )

        w2_scale_chunks = W2g_scales.bitcast(I32).rearrange("(j a) q n -> a j q n", j=QUARTERS)

        def load_w2_scales(a):
            for quadrant in range(4):
                nc.sync.dma_start(
                    out=w2_planes[32 * quadrant : 32 * quadrant + 16, a, :].bitcast(I32),
                    in_=w2_scale_chunks[a][:, 4 * quadrant : 4 * quadrant + 4, :],
                )

        def load_w1_halves(a):
            load_w1(a, 0, 2)
            load_w1(a, 2, QUARTERS)

        def load_w2(a, step):
            w2 = weights.tile([P, QUARTERS, D], U32, align_bytes=64)
            for j in range(0, QUARTERS, step):
                nc.sync.dma_start(
                    out=w2[:, j : j + step, :].bitcast(I32), in_=w2_dram[a][:, j : j + step, :].bitcast(I32)
                )
            w2_tiles[a] = w2

        load_w1(0, 0, 1)
        load_w1_scales(0, HEAD_CHUNKS)
        load_w1(0, 1, QUARTERS)
        for a in range(1, W1_AHEAD):
            load_w1_halves(a)
        load_w1_scales(HEAD_CHUNKS, CHUNKS)
        wv_words = consts.tile([P, D], U32, align_bytes=64)
        for a in range(CHUNKS):
            load_w2_scales(a)
            load_w2(a, 1 if a == CHUNKS - 1 else 2)
            if a == WV_BEHIND:
                for quadrant in range(4):
                    nc.sync.dma_start(
                        out=wv_plane[32 * quadrant : 32 * quadrant + 4, :].bitcast(I32),
                        in_=Wv_scales[0][4 * quadrant : 4 * quadrant + 4, :].bitcast(I32),
                    )
            if a + W1_AHEAD < CHUNKS:
                load_w1_halves(a + W1_AHEAD)
            if a == WV_BEHIND:
                nc.sync.dma_start(
                    out=wv_words[:].bitcast(I32), in_=Wv_words[0].rearrange("p n t -> p (n t)").bitcast(I32)
                )

        x_words = x_sb[:].bitcast(F32).rearrange("p t (q u) -> p t u q", u=2)
        x_grouped = consts.tile([P, TOKENS * PACK], BF16, align_bytes=64)
        for t in range(TOKEN_TILES):
            x_flipped = psum_z.tile([P, 2, P], F32, tag="z")
            for u in range(2):
                nc.tensor.transpose(x_flipped[:, u, :], x_words[:, t, u, :], ident_f32[:])
            nc.scalar.copy(
                out=x_grouped[:, PACK * P * t : PACK * P * (t + 1)].bitcast(F32).rearrange("p (k u) -> p k u", u=2),
                in_=x_flipped[:].rearrange("p u k -> p k u"),
            )

        bias_words = bias_rows[:].bitcast(F32).rearrange("c (q u) -> c u q", u=2)
        bias_flipped = psum_z.tile([P, 2, P], F32, tag="z")
        for u in range(2):
            nc.tensor.transpose(bias_flipped[:, u, :], bias_words[:, u, :], ident_f32[:])
        bias_cols = consts.tile([P, 2, GROUPS], F32)
        nc.scalar.copy(out=bias_cols[:], in_=bias_flipped[:, :, 0:GROUPS])

        x_codes = consts.tile([P, TOKENS], U32, align_bytes=64)
        x_plane = consts.tile([P, TOKENS], U8, align_bytes=64)
        b1_cols = consts.tile([P, GROUPS, PACK], F32)

        tail_bias = consts.tile([P, 2, D], BF16)

        tail_cols = consts.tile([P, 2, 2], F32)
        tail_words = tail_rows[:].bitcast(F32).rearrange("c (q u) -> c u q", u=2)

        def flip_tail_biases():
            for u in range(2):
                nc.tensor.transpose(acc[0][:, P * u : P * (u + 1)], tail_words[:, u, :], ident_f32[:])

        def copy_tail_columns():
            nc.vector.tensor_copy(out=tail_cols[:], in_=acc[0][:, 0 : 2 * P].rearrange("p (u c) -> p u c", u=2)[:, :, 0:2])

        def spread_tail_biases():
            for i in range(2):
                for u in range(2):
                    nc.tensor.transpose(
                        acc[1][:, P * (2 * i + u) : P * (2 * i + u + 1)],
                        tail_cols[:, u, i : i + 1].to_broadcast([P, P]),
                        ident_f32[:],
                    )

        def copy_tail_biases():
            nc.vector.tensor_copy(
                out=tail_bias[:].bitcast(F32).rearrange("p i (q u) -> p i q u", u=2),
                in_=acc[1][:].rearrange("p (i u q) -> p i q u", i=2, u=2),
            )

        w1_sorted = {}
        z_tiles = {}
        h_tiles = {}
        grouped_tiles = {}
        h_codes = {}
        h_planes = {}
        acc = [psum_acc.tile([P, D], F32, name="acc%d" % t) for t in range(TOKEN_TILES)]

        def sort_planes(a):
            nc.vector.tensor_copy(out=w1_planes[:, a, :, :], in_=w1_planes_raw[:, a, :, :].rearrange("p m t -> p t m"))

        def sort_codes(i, count):
            a, j = i // QUARTERS, i % QUARTERS
            w1s = work.tile([P, PACK, count * P], U32, align_bytes=64, bufs=4)
            nc.vector.tensor_copy(
                out=w1s[:].bitcast(I32).rearrange("p t m -> p m t"),
                in_=w1_tiles[a][:, j : j + count, :].rearrange("p j n -> p (j n)").bitcast(I32).rearrange("p (m t) -> p m t", t=PACK),
            )
            for k in range(count):
                w1_sorted[i + k] = w1s[:, :, P * k : P * (k + 1)]

        def first_layer(i):
            a, j = i // QUARTERS, i % QUARTERS
            for half in range(2):
                z = psum_z.tile([P, 2, TOKENS], F32, tag="z")
                for s in range(2):
                    t = 2 * half + s
                    nc.tensor.matmul_mx(
                        out=z[:, s, :],
                        lhsT=w1_sorted[i][:, t, :].bitcast(FP8X4),
                        lhsT_scale=w1_planes[4 * j : P, a, t, :],
                        rhs=x_codes[:].bitcast(FP8X4),
                        rhs_scale=x_plane[:],
                        start=True,
                        stop=True,
                    )
                z_tiles[(i, half)] = z

        def span(i):
            return (i - i % 2, 2) if 4 <= i < GROUPS - 2 else (i, 1)

        def silu(i):
            g = CHUNKS * (i % QUARTERS) + i // QUARTERS
            first, count = span(i)
            if i == first:
                h_tiles[first] = work.tile([P, PACK, count * TOKENS], BF16, name="h")
            pieces = TOKEN_TILES if i == GROUPS - 1 else 1
            width = TOKENS // pieces
            base = TOKENS * (i - first)
            for n0 in range(0, TOKENS, width):
                for t in range(PACK):
                    nc.scalar.activation(
                        out=h_tiles[first][:, t, base + n0 : base + n0 + width],
                        in_=z_tiles[(i, t // 2)][:, t % 2, n0 : n0 + width],
                        func=ACT.Silu,
                        bias=b1_cols[:, g, t : t + 1],
                    )

        def new_tiles(first):
            width = TOKENS * span(first)[1]
            grouped_tiles[first] = work.tile([P, width * PACK], BF16, align_bytes=64, name="grouped")
            h_codes[first] = work.tile([P, width], U32, align_bytes=64, bufs=7, name="codes")
            h_planes[first] = work.tile([P, width], U8, align_bytes=64, bufs=7, name="plane")

        def interleave(first, n0, width):
            nc.vector.tensor_copy(
                out=grouped_tiles[first][:, PACK * n0 : PACK * (n0 + width)].rearrange("p (c i t) -> p c t i", i=4, t=PACK),
                in_=h_tiles[first][:, :, n0 : n0 + width].rearrange("p t (c i) -> p c t i", i=4),
            )

        def quantise(first, n0, width):
            nc.vector.quantize_mx(
                out=h_codes[first][:, n0 : n0 + width].bitcast(FP8X4),
                scales=h_planes[first][:, n0 : n0 + width],
                in_=grouped_tiles[first][:, PACK * n0 : PACK * (n0 + width)],
            )

        def second_layer(i, tiles=(0, 1)):
            a, j = i // QUARTERS, i % QUARTERS
            first = span(i)[0]
            base = TOKENS * (i - first)
            for t in tiles:
                nc.tensor.matmul_mx(
                    out=acc[t][:],
                    lhsT=h_codes[first][:, base + P * t : base + P * (t + 1)].bitcast(FP8X4),
                    lhsT_scale=h_planes[first][:, base + P * t : base + P * (t + 1)],
                    rhs=w2_tiles[a][:, j, :].bitcast(FP8X4),
                    rhs_scale=w2_planes[4 * j : P, a, :],
                    start=(i == 0),
                    stop=(i == GROUPS - 1),
                )

        values = consts.tile([P, TOKEN_TILES, D], F32)
        v_tiles = {}

        def value_product(t):
            v = psum_z.tile([P, D], F32, tag="z")
            nc.tensor.matmul_mx(
                out=v[:],
                lhsT=x_codes[:, P * t : P * (t + 1)].bitcast(FP8X4),
                lhsT_scale=x_plane[:, P * t : P * (t + 1)],
                rhs=wv_words[:].bitcast(FP8X4),
                rhs_scale=wv_plane[:],
                start=True,
                stop=True,
            )
            v_tiles[t] = v

        def value_bias(t):
            nc.vector.tensor_tensor(out=values[:, t, :], in0=v_tiles[t][:], in1=tail_bias[:, 1, :], op=ADD)

        seconds = 0
        quantised = 0
        sorts = {-3: (0, 1), -2: (1, 1), -1: (2, 2)}
        for i in range(4, GROUPS, 2):
            sorts[i - 4] = (i, 2)
        for s in range(-3, GROUPS):
            ready = span(s - 1) if s >= 1 and sum(span(s - 1)) == s else None
            if ready:
                new_tiles(ready[0])
                interleave(ready[0], 0, ready[1] * TOKENS)
            if s in sorts:
                i, count = sorts[s]
                sort_codes(i, count)
                if i % QUARTERS == 0:
                    sort_planes(i // QUARTERS)
                if i == 0:
                    nc.vector.quantize_mx(out=x_codes[:].bitcast(FP8X4), scales=x_plane[:], in_=x_grouped[:])
                    nc.vector.tensor_copy(
                        out=b1_cols[:].rearrange("p c (u e) -> p c u e", u=2),
                        in_=bias_cols[:].bitcast(BF16).rearrange("p u (c e) -> p c u e", e=2),
                    )
            elif s >= GROUPS - 2:
                value_bias(s - (GROUPS - 2))
            if ready:
                quantise(ready[0], 0, ready[1] * TOKENS)
                quantised = ready[0] + ready[1]
            if 0 <= s + 2 < GROUPS - 1:
                first_layer(s + 2)
            elif s + 2 == GROUPS - 1:
                for t in range(TOKEN_TILES):
                    value_product(t)
            elif s + 2 == GROUPS:
                first_layer(GROUPS - 1)
            while seconds < quantised and seconds <= s - SECOND_START:
                second_layer(seconds)
                seconds += 1
            if s >= 0:
                silu(s)
            if s == 5:
                flip_tail_biases()
                copy_tail_columns()
            if s == 6:
                spread_tail_biases()
                copy_tail_biases()
        nc.scalar.activation(out=warm[:], in_=zero[:], func=ACT.Sigmoid)
        for i in range(seconds, GROUPS - QUARTERS):
            second_layer(i)
        last = GROUPS - 1
        for i in range(GROUPS - QUARTERS, last):
            second_layer(i, (0,))
        second_layer(last - 3, (1,))
        new_tiles(last)
        interleave(last, 0, P)
        quantise(last, 0, P)
        second_layer(last, (0,))
        second_layer(last - 2, (1,))
        second_layer(last - 1, (1,))
        interleave(last, P, P)
        quantise(last, P, P)
        second_layer(last, (1,))

        gates = {}
        half = D // 2
        pieces = [(t, c) for t in range(TOKEN_TILES) for c in range(0, D, half)]
        for t, c in pieces:
            gate = work.tile([P, half], F32, bufs=4)
            nc.vector.tensor_tensor(out=gate[:], in0=acc[t][:, c : c + half], in1=tail_bias[:, 0, c : c + half], op=ADD)
            gates[(t, c)] = gate
        for t, c in pieces:
            opened = work.tile([P, half], F32, bufs=4)
            nc.scalar.activation(out=opened[:], in_=gates[(t, c)][:], func=ACT.Sigmoid)
            result = work.tile([P, half], F32, bufs=4)
            nc.vector.tensor_tensor(out=result[:], in0=values[:, t, c : c + half], in1=opened[:], op=MULT)
            nc.sync.dma_start(out=out_rows[P * t : P * (t + 1), c : c + half], in_=result[:])
